import numpy as np
import ml_dtypes


def mxq(x, axis, fmt="e4m3"):
    dtype, down = {"e4m3": (ml_dtypes.float8_e4m3fn, 7), "e5m2": (ml_dtypes.float8_e5m2, 14)}[fmt]
    v = np.moveaxis(np.asarray(x, np.float32).astype(ml_dtypes.bfloat16).astype(np.float64), axis, -1)
    blocks = v.reshape(v.shape[:-1] + (-1, 32))
    amax = np.abs(blocks).max(-1, keepdims=True)
    byte = np.maximum(np.where(amax > 0, np.frexp(amax)[1] - 1 + 127, 0) - down, 1)
    scale = np.exp2(byte - 127.0)
    codes = (blocks / scale).astype(np.float32).astype(dtype).astype(np.float64)
    return np.moveaxis((codes * scale).reshape(v.shape), -1, axis)


WIDE = False


def mx_kscale(k):
    if not WIDE:
        return np.ones(k)
    levels = np.array([10, -10, 5, -5, 0])
    a = np.random.permutation(np.resize(levels, k // 512 * 4)).reshape(k // 512, 4)
    idx = np.arange(k)
    return np.exp2(a[idx // 512, idx % 128 // 32])


BF16 = ml_dtypes.bfloat16


def bf(x):
    return np.asarray(x, np.float32).astype(BF16)


def f64(x):
    return np.asarray(x).astype(np.float64)


E2M1 = np.array([0.0, 0.5, 1.0, 1.5, 2.0, 3.0, 4.0, 6.0, -0.0, -0.5, -1.0, -1.5, -2.0, -3.0, -4.0, -6.0])


def pack_weight(w, fmt):
    k, n = w.shape
    w = f64(bf(w)).reshape(k // 32, 32, n)
    amax = np.abs(w).max(1)
    if fmt == "e4m3":
        byte = np.frexp(amax)[1] - 1 + 127 - 7
    else:
        mant, ex = np.frexp(amax / 6.0)
        byte = np.where(mant > 0.5, ex, ex - 1) + 127
    byte = np.clip(np.where(amax > 0, byte, 1), 1, 254)
    scaled = (w * np.exp2(127.0 - byte)[:, None, :]).reshape(k, n).astype(np.float32)
    by_word = np.ascontiguousarray(scaled.reshape(k // 512, 128, 4, n).transpose(0, 1, 3, 2))
    if fmt == "e4m3":
        words = by_word.astype(ml_dtypes.float8_e4m3fn).view(np.uint8)
    else:
        c = by_word.astype(ml_dtypes.float4_e2m1fn).view(np.uint8) & 0xF
        words = c[..., 0::2] | (c[..., 1::2] << 4)
    return np.ascontiguousarray(words), np.ascontiguousarray(byte.astype(np.uint8).reshape(k // 512, 16, n))


def unpack_weight(words, scales, fmt):
    g, p, n, _ = words.shape
    if fmt == "e4m3":
        vals = np.ascontiguousarray(words).view(ml_dtypes.float8_e4m3fn).astype(np.float64)
    else:
        nib = np.empty((g, p, n, 4), np.uint8)
        nib[..., 0::2] = words & 0xF
        nib[..., 1::2] = words >> 4
        vals = E2M1[nib]
    vals = vals * np.repeat(np.exp2(scales.astype(np.float64) - 127.0), 8, axis=1)[..., None]
    return vals.transpose(0, 1, 3, 2).reshape(g * 512, n)


B, C, H, W = 2, 1024, 32, 32
N = H * W
KV = 0.05 * N / np.sqrt(C)
FMT = "e4m3"


def setup_inputs():
    s, t = mx_kscale(C), mx_kscale(C)
    x = bf(np.random.standard_normal((B, C, H, W)) * s[None, :, None, None])
    mask = bf(np.random.random_sample((B, 1, H, W)))
    W_q_words, W_q_scales = pack_weight(np.random.standard_normal((C, C)) / np.sqrt(C) / s[:, None], FMT)
    b_q = bf(np.random.standard_normal(C) * 0.3)
    kv_know = bf(np.random.standard_normal((B, 1, C)) * KV * t)
    kv_mask = bf(np.random.standard_normal((B, 1, C)) * KV * t)
    W_out_words, W_out_scales = pack_weight(np.random.standard_normal((C, C)) / KV / t[:, None], FMT)
    b_out = bf(np.random.standard_normal(C) * 0.2)
    return {"x": x,
            "mask": mask,
            "W_q_words": W_q_words,
            "W_q_scales": W_q_scales,
            "b_q": b_q,
            "kv_know": kv_know,
            "kv_mask": kv_mask,
            "W_out_words": W_out_words,
            "W_out_scales": W_out_scales,
            "b_out": b_out}


def reference(x, mask, W_q_words, W_q_scales, b_q, kv_know, kv_mask, W_out_words, W_out_scales, b_out):
    x, mask = f64(x), f64(mask)
    b, c, h, w = x.shape
    xf = np.transpose(x, (0, 2, 3, 1)).reshape(b, h * w, c)
    q = (mxq(xf, 2, "e4m3") @ unpack_weight(W_q_words, W_q_scales, FMT)) + f64(b_q)
    q = q / np.linalg.norm(q, axis=-1, keepdims=True)
    m = np.transpose(mask, (0, 2, 3, 1)).reshape(b, h * w, 1)
    inv = 1.0 - m
    qu = q * inv
    qm = q * m
    out_know = f64(kv_know) * qu
    out_mask = f64(kv_mask) * qm
    out = out_know * inv + m * (0.3 * out_know + 0.7 * out_mask)
    return (mxq(out, 2, "e4m3") @ unpack_weight(W_out_words, W_out_scales, FMT)) + f64(b_out)

@@ -1,0 +1,235 @@
+from contextlib import ExitStack
+
+import concourse.mybir as mybir
+from concourse.masks import make_identity
+
+F32 = mybir.dt.float32
+BF16 = mybir.dt.bfloat16
+I32 = mybir.dt.int32
+U32 = mybir.dt.uint32
+U8 = mybir.dt.uint8
+FP8X4 = mybir.dt.float8_e4m3fn_x4
+ALU = mybir.AluOpType
+ACT = mybir.ActivationFunctionType
+
+P = 128
+PACK = 4
+K_PASS = P * PACK
+IMAGES = 2
+PIXELS = 1024
+CHANNELS = 1024
+GROUPS = CHANNELS // K_PASS
+BANK = 512
+HALVES = CHANNELS // BANK
+TILES_PER_IMAGE = PIXELS // P
+TILES = IMAGES * TILES_PER_IMAGE
+CHUNK = 512
+TILES_PER_CHUNK = CHUNK // P
+PIECES = 3
+PLANE_ROWS = 4
+
+FLOPS = 2 * 2 * IMAGES * PIXELS * CHANNELS * CHANNELS
+
+
+def tile_hydraattention_pb_kernel(
+    tc, x, mask, W_q_words, W_q_scales, b_q, kv_know, kv_mask, W_out_words, W_out_scales, b_out, out
+):
+    nc = tc.nc
+    with ExitStack() as ctx:
+        keep = ctx.enter_context(tc.tile_pool(name="keep", bufs=1))
+        small = ctx.enter_context(tc.tile_pool(name="small", bufs=4))
+        work = ctx.enter_context(tc.tile_pool(name="work", bufs=3))
+        psum = ctx.enter_context(tc.psum_pool(name="psum", bufs=2))
+
+        x_raw = {}
+
+        def load_x(image, chunk):
+            for g in range(GROUPS):
+                raw = keep.tile([P, PACK, CHUNK], BF16, name="x_raw_%d_%d_%d" % (image, chunk, g))
+                rows = x[image, g * K_PASS : (g + 1) * K_PASS].rearrange("(p j) r w -> p j (r w)", j=PACK)
+                nc.sync.dma_start(out=raw[:], in_=rows[:, :, chunk * CHUNK : (chunk + 1) * CHUNK])
+                x_raw[(image, chunk, g)] = raw
+
+        planes = keep.tile([P, CHANNELS], U8, align_bytes=64)
+        nc.vector.memset(planes[:].bitcast(I32), 0)
+
+        def load_weight(words_in, scales_in, first_plane, name):
+            for quadrant in range(4):
+                top = 32 * quadrant + PLANE_ROWS * first_plane
+                nc.sync.dma_start(
+                    out=planes[top : top + GROUPS * PLANE_ROWS, :].bitcast(I32),
+                    in_=scales_in[:, PLANE_ROWS * quadrant : PLANE_ROWS * (quadrant + 1), :].bitcast(I32),
+                )
+            words = keep.tile([P, GROUPS, CHANNELS], U32, name=name, align_bytes=64)
+            for g in range(GROUPS):
+                nc.sync.dma_start(
+                    out=words[:, g, :].bitcast(I32),
+                    in_=words_in[g].rearrange("p n t -> p (n t)").bitcast(I32),
+                )
+            return words
+
+        def scale_plane(number, cols):
+            return planes[PLANE_ROWS * number : P, cols]
+
+        load_x(0, 0)
+        wq_words = load_weight(W_q_words, W_q_scales, 0, "wq_words")
+        load_x(0, 1)
+        wo_words = load_weight(W_out_words, W_out_scales, GROUPS, "wo_words")
+        load_x(1, 0)
+        load_x(1, 1)
+
+        mask_rows = keep.tile([P, P], BF16)
+        nc.vector.memset(mask_rows[:], 0.0)
+        nc.scalar.dma_start(
+            out=mask_rows[0:TILES, :],
+            in_=mask.rearrange("b o (i r) w -> (b o i) (r w)", i=TILES_PER_IMAGE),
+        )
+        bq_all = keep.tile([P, CHANNELS], BF16)
+        nc.scalar.dma_start(out=bq_all[:], in_=b_q.partition_broadcast(P))
+        kv_rows = []
+        for image in range(IMAGES):
+            rows = keep.tile([P, CHANNELS], BF16, name="kv_rows_%d" % image)
+            nc.vector.memset(rows[:], 0.0)
+            nc.scalar.dma_start(out=rows[0:PIECES, :], in_=kv_know[image, 0].partition_broadcast(PIECES))
+            nc.scalar.dma_start(out=rows[PIECES : 2 * PIECES, :], in_=kv_mask[image, 0].partition_broadcast(PIECES))
+            kv_rows.append(rows)
+        bo_all = keep.tile([P, CHANNELS], BF16)
+        nc.scalar.dma_start(out=bo_all[:], in_=b_out.partition_broadcast(P))
+
+        ident_bf = keep.tile([P, P], BF16)
+        make_identity(nc, ident_bf[:])
+        ident_f32 = keep.tile([P, P], F32)
+        make_identity(nc, ident_f32[:])
+
+        mask_ps = psum.tile([P, P], BF16, tag="turned")
+        nc.tensor.transpose(mask_ps[:], mask_rows[:], ident_bf[:])
+        m = keep.tile([P, TILES], F32)
+        nc.vector.tensor_copy(out=m[:], in_=mask_ps[:, 0:TILES])
+        inv = keep.tile([P, TILES], F32)
+        nc.vector.tensor_scalar(out=inv[:], in0=m[:], scalar1=-1.0, scalar2=1.0, op0=ALU.mult, op1=ALU.add)
+        blend = keep.tile([P, TILES], F32)
+        nc.vector.scalar_tensor_tensor(out=blend[:], in0=m[:], scalar=0.3, in1=inv[:], op0=ALU.mult, op1=ALU.add)
+        know_w = keep.tile([P, TILES], F32)
+        nc.vector.tensor_tensor(out=know_w[:], in0=inv[:], in1=blend[:], op=ALU.mult)
+        mask_w = keep.tile([P, TILES], F32)
+        nc.vector.scalar_tensor_tensor(out=mask_w[:], in0=m[:], scalar=0.7, in1=m[:], op0=ALU.mult, op1=ALU.mult)
+
+        weight_cols = keep.tile([P, TILES, P], BF16)
+        nc.vector.memset(weight_cols[:], 0.0)
+        for first_row, weight in ((0, know_w), (PIECES, mask_w)):
+            rest = weight
+            for piece in range(PIECES):
+                column = weight_cols[:, :, first_row + piece]
+                nc.vector.tensor_copy(out=column, in_=rest[:])
+                if piece < PIECES - 1:
+                    smaller = keep.tile([P, TILES], F32, name="rest_%d_%d" % (first_row, piece))
+                    nc.vector.tensor_tensor(out=smaller[:], in0=rest[:], in1=column, op=ALU.subtract)
+                    rest = smaller
+        weight_rows = keep.tile([P, TILES, P], BF16)
+        per_bank = 2 * BANK // P
+        for first in range(0, TILES, per_bank):
+            rows_ps = psum.tile([P, per_bank, P], BF16, tag="turned")
+            for i in range(per_bank):
+                nc.tensor.transpose(rows_ps[:, i, :], weight_cols[:, first + i, :], ident_bf[:])
+            nc.vector.tensor_copy(out=weight_rows[:, first : first + per_bank, :], in_=rows_ps[:])
+
+        x_mx = {}
+        q_of = {}
+        g_mx = {}
+
+        def quantise_x(tile_no):
+            image, in_image = divmod(tile_no, TILES_PER_IMAGE)
+            chunk, in_chunk = divmod(in_image, TILES_PER_CHUNK)
+            pixels = slice(in_chunk * P, (in_chunk + 1) * P)
+            x_grouped = work.tile([P, GROUPS, P, PACK], BF16, align_bytes=64)
+            for g in range(GROUPS):
+                nc.scalar.copy(
+                    out=x_grouped[:, g].rearrange("p (c i) j -> p c j i", i=4),
+                    in_=x_raw[(image, chunk, g)][:, :, pixels].rearrange("p j (c i) -> p c j i", i=4),
+                )
+            x_codes = work.tile([P, GROUPS * P], U32, align_bytes=64)
+            x_scales = work.tile([P, GROUPS * P], U8, align_bytes=64)
+            nc.vector.quantize_mx(
+                out=x_codes[:].bitcast(FP8X4),
+                scales=x_scales[:],
+                in_=x_grouped[:].rearrange("p g w j -> p (g w j)"),
+            )
+            x_mx[tile_no] = (x_codes, x_scales)
+
+        def project(acc, codes, scales, words, first_plane, cols):
+            for g in range(GROUPS):
+                nc.tensor.matmul_mx(
+                    out=acc[:],
+                    lhsT=codes[:, g * P : (g + 1) * P].bitcast(FP8X4),
+                    lhsT_scale=scales[:, g * P : (g + 1) * P],
+                    rhs=words[:, g, cols].bitcast(FP8X4),
+                    rhs_scale=scale_plane(first_plane + g, cols),
+                    start=(g == 0),
+                    stop=(g == GROUPS - 1),
+                )
+
+        def queries(tile_no):
+            x_codes, x_scales = x_mx[tile_no]
+            q = work.tile([P, CHANNELS], F32)
+            for half in range(HALVES):
+                cols = slice(half * BANK, (half + 1) * BANK)
+                q_ps = psum.tile([P, BANK], F32)
+                project(q_ps, x_codes, x_scales, wq_words, 0, cols)
+                nc.vector.tensor_tensor(out=q[:, cols], in0=q_ps[:], in1=bq_all[:, cols], op=ALU.add)
+            squares = work.tile([P, CHANNELS], BF16)
+            sum_sq = small.tile([P, 1], F32)
+            nc.scalar.activation(out=squares[:], in_=q[:], func=ACT.Square, accum_out=sum_sq[:])
+            norm = small.tile([P, 1], F32)
+            nc.scalar.activation(out=norm[:], in_=sum_sq[:], func=ACT.Sqrt)
+            inv_norm = small.tile([P, 1], F32)
+            nc.vector.reciprocal(out=inv_norm[:], in_=norm[:])
+            q_of[tile_no] = (q, inv_norm)
+
+        def gate(tile_no):
+            image = tile_no // TILES_PER_IMAGE
+            q, inv_norm = q_of[tile_no]
+            g_rows = work.tile([P, CHANNELS], BF16)
+            for half in range(HALVES):
+                cols = slice(half * BANK, (half + 1) * BANK)
+                gate_ps = psum.tile([P, BANK], F32)
+                nc.tensor.matmul(
+                    out=gate_ps[:], lhsT=weight_rows[:, tile_no, :], rhs=kv_rows[image][:, cols], start=True, stop=True
+                )
+                nc.vector.scalar_tensor_tensor(
+                    out=g_rows[:, cols], in0=q[:, cols], scalar=inv_norm[:, 0:1], in1=gate_ps[:],
+                    op0=ALU.mult, op1=ALU.mult,
+                )
+            pairs = g_rows[:].bitcast(F32)
+            pair_cols = K_PASS // 2
+            turned = psum.tile([P, GROUPS, 2, P], F32)
+            for g in range(GROUPS):
+                for u in range(2):
+                    nc.tensor.transpose(
+                        turned[:, g, u, :], pairs[:, g * pair_cols + u : (g + 1) * pair_cols : 2], ident_f32[:]
+                    )
+            g_grouped = work.tile([P, CHANNELS], BF16, align_bytes=64)
+            nc.scalar.copy(
+                out=g_grouped[:].bitcast(F32).rearrange("p (g w u) -> p g w u", g=GROUPS, u=2),
+                in_=turned[:].rearrange("p g u w -> p g w u"),
+            )
+            g_codes = work.tile([P, GROUPS * P], U32, align_bytes=64)
+            g_scales = work.tile([P, GROUPS * P], U8, align_bytes=64)
+            nc.vector.quantize_mx(out=g_codes[:].bitcast(FP8X4), scales=g_scales[:], in_=g_grouped[:])
+            g_mx[tile_no] = (g_codes, g_scales)
+
+        def outputs(tile_no):
+            image, in_image = divmod(tile_no, TILES_PER_IMAGE)
+            g_codes, g_scales = g_mx[tile_no]
+            y = work.tile([P, CHANNELS], F32)
+            for half in range(HALVES):
+                cols = slice(half * BANK, (half + 1) * BANK)
+                y_ps = psum.tile([P, BANK], F32)
+                project(y_ps, g_codes, g_scales, wo_words, GROUPS, cols)
+                nc.vector.tensor_tensor(out=y[:, cols], in0=y_ps[:], in1=bo_all[:, cols], op=ALU.add)
+            nc.sync.dma_start(out=out[image, in_image * P : (in_image + 1) * P, :], in_=y[:])
+
+        stages = (quantise_x, queries, gate, outputs)
+        for step in range(TILES + len(stages) - 1):
+            for lag, stage in enumerate(stages):
+                if 0 <= step - lag < TILES:
+                    stage(step - lag)

@@ -84,8 +84,9 @@ def tile_hydraattention_pb_kernel(
             out=mask_rows[0:TILES, :],
             in_=mask.rearrange("b o (i r) w -> (b o i) (r w)", i=TILES_PER_IMAGE),
         )
-        bq_all = keep.tile([P, CHANNELS], BF16)
-        nc.scalar.dma_start(out=bq_all[:], in_=b_q.partition_broadcast(P))
+        bias_rows = keep.tile([P, 2, CHANNELS], BF16)
+        nc.vector.memset(bias_rows[:], 0.0)
+        nc.scalar.dma_start(out=bias_rows[0:1, 0, :], in_=b_q.unsqueeze(0))
         kv_rows = []
         for image in range(IMAGES):
             rows = keep.tile([P, CHANNELS], BF16, name="kv_rows_%d" % image)
@@ -93,8 +94,12 @@ def tile_hydraattention_pb_kernel(
             nc.scalar.dma_start(out=rows[0:PIECES, :], in_=kv_know[image, 0].partition_broadcast(PIECES))
             nc.scalar.dma_start(out=rows[PIECES : 2 * PIECES, :], in_=kv_mask[image, 0].partition_broadcast(PIECES))
             kv_rows.append(rows)
-        bo_all = keep.tile([P, CHANNELS], BF16)
-        nc.scalar.dma_start(out=bo_all[:], in_=b_out.partition_broadcast(P))
+        nc.scalar.dma_start(out=bias_rows[0:1, 1, :], in_=b_out.unsqueeze(0))
+
+        one = keep.tile([P, 1], F32)
+        nc.vector.memset(one[:], 1.0)
+        warm = keep.tile([P, 1], F32)
+        nc.scalar.activation(out=warm[:], in_=one[:], func=ACT.Sqrt)
 
         ident_bf = keep.tile([P, P], BF16)
         make_identity(nc, ident_bf[:])
@@ -133,11 +138,28 @@ def tile_hydraattention_pb_kernel(
                 nc.tensor.transpose(rows_ps[:, i, :], weight_cols[:, first + i, :], ident_bf[:])
             nc.vector.tensor_copy(out=weight_rows[:, first : first + per_bank, :], in_=rows_ps[:])
 
-        x_mx = {}
-        q_of = {}
-        g_mx = {}
+        ones = keep.tile([P, P], BF16)
+        nc.vector.memset(ones[:], 1.0)
+        bq_all = keep.tile([P, CHANNELS], BF16)
+        bo_all = keep.tile([P, CHANNELS], BF16)
+        for which, bias_all in enumerate((bq_all, bo_all)):
+            for half in range(HALVES):
+                cols = slice(half * BANK, (half + 1) * BANK)
+                bias_ps = psum.tile([P, BANK], F32, tag="gate_ps")
+                nc.tensor.matmul(out=bias_ps[:], lhsT=ones[:], rhs=bias_rows[:, which, cols], start=True, stop=True)
+                nc.scalar.copy(out=bias_all[:, cols], in_=bias_ps[:])
 
-        def quantise_x(tile_no):
+        x_grouped_of = {}
+        x_mx = {}
+        q_banks = {}
+        q_of = {}
+        gate_banks = {}
+        g_rows_of = {}
+        g_grouped_of = {}
+        g_mx = {}
+        y_banks = {}
+
+        def regroup_x(tile_no):
             image, in_image = divmod(tile_no, TILES_PER_IMAGE)
             chunk, in_chunk = divmod(in_image, TILES_PER_CHUNK)
             pixels = slice(in_chunk * P, (in_chunk + 1) * P)
@@ -147,59 +169,78 @@ def tile_hydraattention_pb_kernel(
                     out=x_grouped[:, g].rearrange("p (c i) j -> p c j i", i=4),
                     in_=x_raw[(image, chunk, g)][:, :, pixels].rearrange("p j (c i) -> p c j i", i=4),
                 )
-            x_codes = work.tile([P, GROUPS * P], U32, align_bytes=64)
-            x_scales = work.tile([P, GROUPS * P], U8, align_bytes=64)
-            nc.vector.quantize_mx(
-                out=x_codes[:].bitcast(FP8X4),
-                scales=x_scales[:],
-                in_=x_grouped[:].rearrange("p g w j -> p (g w j)"),
-            )
-            x_mx[tile_no] = (x_codes, x_scales)
+            x_grouped_of[tile_no] = x_grouped
 
-        def project(acc, codes, scales, words, first_plane, cols):
-            for g in range(GROUPS):
-                nc.tensor.matmul_mx(
-                    out=acc[:],
-                    lhsT=codes[:, g * P : (g + 1) * P].bitcast(FP8X4),
-                    lhsT_scale=scales[:, g * P : (g + 1) * P],
-                    rhs=words[:, g, cols].bitcast(FP8X4),
-                    rhs_scale=scale_plane(first_plane + g, cols),
-                    start=(g == 0),
-                    stop=(g == GROUPS - 1),
-                )
+        def quantise(grouped, what):
+            codes = work.tile([P, GROUPS * P], U32, tag=what + "_codes", align_bytes=64)
+            scales = work.tile([P, GROUPS * P], U8, tag=what + "_scales", align_bytes=64)
+            nc.vector.quantize_mx(out=codes[:].bitcast(FP8X4), scales=scales[:], in_=grouped)
+            return codes, scales
 
-        def queries(tile_no):
-            x_codes, x_scales = x_mx[tile_no]
+        def quantise_x(tile_no):
+            x_mx[tile_no] = quantise(x_grouped_of[tile_no][:].rearrange("p g w j -> p (g w j)"), "x")
+
+        def project(operand, words, first_plane, tag):
+            codes, scales = operand
+            banks = []
+            for half in range(HALVES):
+                cols = slice(half * BANK, (half + 1) * BANK)
+                acc = psum.tile([P, BANK], F32, tag=tag)
+                for g in range(GROUPS):
+                    nc.tensor.matmul_mx(
+                        out=acc[:],
+                        lhsT=codes[:, g * P : (g + 1) * P].bitcast(FP8X4),
+                        lhsT_scale=scales[:, g * P : (g + 1) * P],
+                        rhs=words[:, g, cols].bitcast(FP8X4),
+                        rhs_scale=scale_plane(first_plane + g, cols),
+                        start=(g == 0),
+                        stop=(g == GROUPS - 1),
+                    )
+                banks.append(acc)
+            return banks
+
+        def queries_mm(tile_no):
+            q_banks[tile_no] = project(x_mx[tile_no], wq_words, 0, "q_ps")
+
+        def queries_exit(tile_no):
             q = work.tile([P, CHANNELS], F32)
             for half in range(HALVES):
                 cols = slice(half * BANK, (half + 1) * BANK)
-                q_ps = psum.tile([P, BANK], F32)
-                project(q_ps, x_codes, x_scales, wq_words, 0, cols)
-                nc.vector.tensor_tensor(out=q[:, cols], in0=q_ps[:], in1=bq_all[:, cols], op=ALU.add)
+                nc.vector.tensor_tensor(out=q[:, cols], in0=q_banks[tile_no][half][:], in1=bq_all[:, cols], op=ALU.add)
             squares = work.tile([P, CHANNELS], BF16)
             sum_sq = small.tile([P, 1], F32)
             nc.scalar.activation(out=squares[:], in_=q[:], func=ACT.Square, accum_out=sum_sq[:])
             norm = small.tile([P, 1], F32)
             nc.scalar.activation(out=norm[:], in_=sum_sq[:], func=ACT.Sqrt)
-            inv_norm = small.tile([P, 1], F32)
-            nc.vector.reciprocal(out=inv_norm[:], in_=norm[:])
-            q_of[tile_no] = (q, inv_norm)
+            q_of[tile_no] = (q, norm)
 
-        def gate(tile_no):
+        def gate_mm(tile_no):
             image = tile_no // TILES_PER_IMAGE
-            q, inv_norm = q_of[tile_no]
-            g_rows = work.tile([P, CHANNELS], BF16)
+            banks = []
             for half in range(HALVES):
                 cols = slice(half * BANK, (half + 1) * BANK)
                 gate_ps = psum.tile([P, BANK], F32)
                 nc.tensor.matmul(
                     out=gate_ps[:], lhsT=weight_rows[:, tile_no, :], rhs=kv_rows[image][:, cols], start=True, stop=True
                 )
+                banks.append(gate_ps)
+            gate_banks[tile_no] = banks
+
+        def gate_apply(tile_no):
+            q, norm = q_of[tile_no]
+            inv_norm = small.tile([P, 1], F32)
+            nc.vector.reciprocal(out=inv_norm[:], in_=norm[:])
+            g_rows = work.tile([P, CHANNELS], BF16)
+            for half in range(HALVES):
+                cols = slice(half * BANK, (half + 1) * BANK)
                 nc.vector.scalar_tensor_tensor(
-                    out=g_rows[:, cols], in0=q[:, cols], scalar=inv_norm[:, 0:1], in1=gate_ps[:],
+                    out=g_rows[:, cols], in0=q[:, cols], scalar=inv_norm[:, 0:1], in1=gate_banks[tile_no][half][:],
                     op0=ALU.mult, op1=ALU.mult,
                 )
-            pairs = g_rows[:].bitcast(F32)
+            g_rows_of[tile_no] = g_rows
+
+        def turn(tile_no):
+            pairs = g_rows_of[tile_no][:].bitcast(F32)
             pair_cols = K_PASS // 2
             turned = psum.tile([P, GROUPS, 2, P], F32)
             for g in range(GROUPS):
@@ -212,24 +253,35 @@ def tile_hydraattention_pb_kernel(
                 out=g_grouped[:].bitcast(F32).rearrange("p (g w u) -> p g w u", g=GROUPS, u=2),
                 in_=turned[:].rearrange("p g u w -> p g w u"),
             )
-            g_codes = work.tile([P, GROUPS * P], U32, align_bytes=64)
-            g_scales = work.tile([P, GROUPS * P], U8, align_bytes=64)
-            nc.vector.quantize_mx(out=g_codes[:].bitcast(FP8X4), scales=g_scales[:], in_=g_grouped[:])
-            g_mx[tile_no] = (g_codes, g_scales)
+            g_grouped_of[tile_no] = g_grouped
 
-        def outputs(tile_no):
+        def quantise_g(tile_no):
+            g_mx[tile_no] = quantise(g_grouped_of[tile_no][:], "g")
+
+        def outputs_mm(tile_no):
+            y_banks[tile_no] = project(g_mx[tile_no], wo_words, GROUPS, "y_ps")
+
+        def outputs_exit(tile_no):
             image, in_image = divmod(tile_no, TILES_PER_IMAGE)
-            g_codes, g_scales = g_mx[tile_no]
             y = work.tile([P, CHANNELS], F32)
             for half in range(HALVES):
                 cols = slice(half * BANK, (half + 1) * BANK)
-                y_ps = psum.tile([P, BANK], F32)
-                project(y_ps, g_codes, g_scales, wo_words, GROUPS, cols)
-                nc.vector.tensor_tensor(out=y[:, cols], in0=y_ps[:], in1=bo_all[:, cols], op=ALU.add)
+                nc.vector.tensor_tensor(out=y[:, cols], in0=y_banks[tile_no][half][:], in1=bo_all[:, cols], op=ALU.add)
             nc.sync.dma_start(out=out[image, in_image * P : (in_image + 1) * P, :], in_=y[:])
 
-        stages = (quantise_x, queries, gate, outputs)
-        for step in range(TILES + len(stages) - 1):
-            for lag, stage in enumerate(stages):
-                if 0 <= step - lag < TILES:
-                    stage(step - lag)
+        def run(stage, tile_no):
+            if 0 <= tile_no < TILES:
+                stage(tile_no)
+
+        with tc.manual_schedule():
+            for s in range(-4, TILES + 3):
+                run(outputs_exit, s - 3)
+                run(outputs_mm, s - 2)
+                run(queries_exit, s + 1)
+                run(queries_mm, s + 2)
+                run(gate_apply, s)
+                run(gate_mm, s + 1)
+                run(turn, s)
+                run(quantise_g, s - 1)
+                run(regroup_x, s + 4)
+                run(quantise_x, s + 3)

@@ -266,7 +266,11 @@ def tile_hydraattention_pb_kernel(
             y = work.tile([P, CHANNELS], F32)
             for half in range(HALVES):
                 cols = slice(half * BANK, (half + 1) * BANK)
-                nc.vector.tensor_tensor(out=y[:, cols], in0=y_banks[tile_no][half][:], in1=bo_all[:, cols], op=ALU.add)
+                if tile_no % 2 == 0:
+                    nc.vector.tensor_tensor(out=y[:, cols], in0=y_banks[tile_no][half][:], in1=bo_all[:, cols], op=ALU.add)
+                else:
+                    nc.scalar.copy(out=y[:, cols], in_=y_banks[tile_no][half][:])
+                    nc.gpsimd.tensor_tensor(out=y[:, cols], in0=y[:, cols], in1=bo_all[:, cols], op=ALU.add)
             nc.sync.dma_start(out=out[image, in_image * P : (in_image + 1) * P, :], in_=y[:])
 
         def run(stage, tile_no):

@@ -23,12 +23,17 @@ BANK = 512
 HALVES = CHANNELS // BANK
 TILES_PER_IMAGE = PIXELS // P
 TILES = IMAGES * TILES_PER_IMAGE
-CHUNK = 512
+CHUNK = 256
+CHUNKS = PIXELS // CHUNK
 TILES_PER_CHUNK = CHUNK // P
 PIECES = 3
 PLANE_ROWS = 4
 
 FLOPS = 2 * 2 * IMAGES * PIXELS * CHANNELS * CHANNELS
+
+
+def half_cols(half):
+    return slice(half * BANK, (half + 1) * BANK)
 
 
 def tile_hydraattention_pb_kernel(
@@ -40,6 +45,18 @@ def tile_hydraattention_pb_kernel(
         small = ctx.enter_context(tc.tile_pool(name="small", bufs=4))
         work = ctx.enter_context(tc.tile_pool(name="work", bufs=3))
         psum = ctx.enter_context(tc.psum_pool(name="psum", bufs=2))
+        ctx.enter_context(tc.manual_schedule())
+
+
+        mask_rows = keep.tile([P, P], BF16)
+        nc.vector.memset(mask_rows[:], 0.0)
+        nc.sync.dma_start(
+            out=mask_rows[0:TILES, :],
+            in_=mask.rearrange("b o (i r) w -> (b o i) (r w)", i=TILES_PER_IMAGE),
+        )
+        bq_row = keep.tile([P, CHANNELS], BF16)
+        nc.vector.memset(bq_row[:], 0.0)
+        nc.sync.dma_start(out=bq_row[0:1, :], in_=b_q.unsqueeze(0))
 
         x_raw = {}
 
@@ -61,11 +78,12 @@ def tile_hydraattention_pb_kernel(
                     in_=scales_in[:, PLANE_ROWS * quadrant : PLANE_ROWS * (quadrant + 1), :].bitcast(I32),
                 )
             words = keep.tile([P, GROUPS, CHANNELS], U32, name=name, align_bytes=64)
-            for g in range(GROUPS):
-                nc.sync.dma_start(
-                    out=words[:, g, :].bitcast(I32),
-                    in_=words_in[g].rearrange("p n t -> p (n t)").bitcast(I32),
-                )
+            for half in range(HALVES):
+                for g in range(GROUPS):
+                    nc.sync.dma_start(
+                        out=words[:, g, half_cols(half)].bitcast(I32),
+                        in_=words_in[g, :, half_cols(half), :].rearrange("p n t -> p (n t)").bitcast(I32),
+                    )
             return words
 
         def scale_plane(number, cols):
@@ -75,18 +93,14 @@ def tile_hydraattention_pb_kernel(
         wq_words = load_weight(W_q_words, W_q_scales, 0, "wq_words")
         load_x(0, 1)
         wo_words = load_weight(W_out_words, W_out_scales, GROUPS, "wo_words")
-        load_x(1, 0)
-        load_x(1, 1)
+        for chunk in range(2, CHUNKS):
+            load_x(0, chunk)
+        for chunk in range(CHUNKS):
+            load_x(1, chunk)
 
-        mask_rows = keep.tile([P, P], BF16)
-        nc.vector.memset(mask_rows[:], 0.0)
-        nc.scalar.dma_start(
-            out=mask_rows[0:TILES, :],
-            in_=mask.rearrange("b o (i r) w -> (b o i) (r w)", i=TILES_PER_IMAGE),
-        )
-        bias_rows = keep.tile([P, 2, CHANNELS], BF16)
-        nc.vector.memset(bias_rows[:], 0.0)
-        nc.scalar.dma_start(out=bias_rows[0:1, 0, :], in_=b_q.unsqueeze(0))
+        bo_row = keep.tile([P, CHANNELS], BF16)
+        nc.vector.memset(bo_row[:], 0.0)
+        nc.scalar.dma_start(out=bo_row[0:1, :], in_=b_out.unsqueeze(0))
         kv_rows = []
         for image in range(IMAGES):
             rows = keep.tile([P, CHANNELS], BF16, name="kv_rows_%d" % image)
@@ -94,19 +108,21 @@ def tile_hydraattention_pb_kernel(
             nc.scalar.dma_start(out=rows[0:PIECES, :], in_=kv_know[image, 0].partition_broadcast(PIECES))
             nc.scalar.dma_start(out=rows[PIECES : 2 * PIECES, :], in_=kv_mask[image, 0].partition_broadcast(PIECES))
             kv_rows.append(rows)
-        nc.scalar.dma_start(out=bias_rows[0:1, 1, :], in_=b_out.unsqueeze(0))
-
-        one = keep.tile([P, 1], F32)
-        nc.vector.memset(one[:], 1.0)
-        warm = keep.tile([P, 1], F32)
-        nc.scalar.activation(out=warm[:], in_=one[:], func=ACT.Sqrt)
 
         ident_bf = keep.tile([P, P], BF16)
         make_identity(nc, ident_bf[:])
         ident_f32 = keep.tile([P, P], F32)
         make_identity(nc, ident_f32[:])
+        ones = keep.tile([P, P], BF16)
+        nc.vector.memset(ones[:], 1.0)
+        minus_half = keep.tile([P, 1], F32)
+        nc.vector.memset(minus_half[:], -0.5)
+        weight_cols = keep.tile([P, TILES, P], BF16)
+        nc.vector.memset(weight_cols[:], 0.0)
+        warm = keep.tile([P, 1], F32)
+        nc.scalar.activation(out=warm[:], in_=minus_half[:], func=ACT.Square)
 
-        mask_ps = psum.tile([P, P], BF16, tag="turned")
+        mask_ps = psum.tile([P, P], BF16, tag="weight_ps", bufs=1)
         nc.tensor.transpose(mask_ps[:], mask_rows[:], ident_bf[:])
         m = keep.tile([P, TILES], F32)
         nc.vector.tensor_copy(out=m[:], in_=mask_ps[:, 0:TILES])
@@ -119,8 +135,6 @@ def tile_hydraattention_pb_kernel(
         mask_w = keep.tile([P, TILES], F32)
         nc.vector.scalar_tensor_tensor(out=mask_w[:], in0=m[:], scalar=0.7, in1=m[:], op0=ALU.mult, op1=ALU.mult)
 
-        weight_cols = keep.tile([P, TILES, P], BF16)
-        nc.vector.memset(weight_cols[:], 0.0)
         for first_row, weight in ((0, know_w), (PIECES, mask_w)):
             rest = weight
             for piece in range(PIECES):
@@ -130,29 +144,23 @@ def tile_hydraattention_pb_kernel(
                     smaller = keep.tile([P, TILES], F32, name="rest_%d_%d" % (first_row, piece))
                     nc.vector.tensor_tensor(out=smaller[:], in0=rest[:], in1=column, op=ALU.subtract)
                     rest = smaller
-        weight_rows = keep.tile([P, TILES, P], BF16)
-        per_bank = 2 * BANK // P
-        for first in range(0, TILES, per_bank):
-            rows_ps = psum.tile([P, per_bank, P], BF16, tag="turned")
-            for i in range(per_bank):
-                nc.tensor.transpose(rows_ps[:, i, :], weight_cols[:, first + i, :], ident_bf[:])
-            nc.vector.tensor_copy(out=weight_rows[:, first : first + per_bank, :], in_=rows_ps[:])
 
-        ones = keep.tile([P, P], BF16)
-        nc.vector.memset(ones[:], 1.0)
-        bq_all = keep.tile([P, CHANNELS], BF16)
-        bo_all = keep.tile([P, CHANNELS], BF16)
-        for which, bias_all in enumerate((bq_all, bo_all)):
+        def spread(bias_row, name):
+            bias_all = keep.tile([P, CHANNELS], BF16, name=name)
             for half in range(HALVES):
-                cols = slice(half * BANK, (half + 1) * BANK)
                 bias_ps = psum.tile([P, BANK], F32, tag="gate_ps")
-                nc.tensor.matmul(out=bias_ps[:], lhsT=ones[:], rhs=bias_rows[:, which, cols], start=True, stop=True)
-                nc.scalar.copy(out=bias_all[:, cols], in_=bias_ps[:])
+                nc.tensor.matmul(out=bias_ps[:], lhsT=ones[:], rhs=bias_row[:, half_cols(half)], start=True, stop=True)
+                nc.scalar.copy(out=bias_all[:, half_cols(half)], in_=bias_ps[:])
+            return bias_all
+
+        bq_all = spread(bq_row, "bq_all")
+        bo_all = spread(bo_row, "bo_all")
 
         x_grouped_of = {}
         x_mx = {}
         q_banks = {}
         q_of = {}
+        weight_rows_of = {}
         gate_banks = {}
         g_rows_of = {}
         g_grouped_of = {}
@@ -163,9 +171,10 @@ def tile_hydraattention_pb_kernel(
             image, in_image = divmod(tile_no, TILES_PER_IMAGE)
             chunk, in_chunk = divmod(in_image, TILES_PER_CHUNK)
             pixels = slice(in_chunk * P, (in_chunk + 1) * P)
+            copy = nc.vector.tensor_copy if tile_no < TILES_PER_CHUNK else nc.scalar.copy
             x_grouped = work.tile([P, GROUPS, P, PACK], BF16, align_bytes=64)
             for g in range(GROUPS):
-                nc.scalar.copy(
+                copy(
                     out=x_grouped[:, g].rearrange("p (c i) j -> p c j i", i=4),
                     in_=x_raw[(image, chunk, g)][:, :, pixels].rearrange("p j (c i) -> p c j i", i=4),
                 )
@@ -184,15 +193,14 @@ def tile_hydraattention_pb_kernel(
             codes, scales = operand
             banks = []
             for half in range(HALVES):
-                cols = slice(half * BANK, (half + 1) * BANK)
                 acc = psum.tile([P, BANK], F32, tag=tag)
                 for g in range(GROUPS):
                     nc.tensor.matmul_mx(
                         out=acc[:],
                         lhsT=codes[:, g * P : (g + 1) * P].bitcast(FP8X4),
                         lhsT_scale=scales[:, g * P : (g + 1) * P],
-                        rhs=words[:, g, cols].bitcast(FP8X4),
-                        rhs_scale=scale_plane(first_plane + g, cols),
+                        rhs=words[:, g, half_cols(half)].bitcast(FP8X4),
+                        rhs_scale=scale_plane(first_plane + g, half_cols(half)),
                         start=(g == 0),
                         stop=(g == GROUPS - 1),
                     )
@@ -205,34 +213,39 @@ def tile_hydraattention_pb_kernel(
         def queries_exit(tile_no):
             q = work.tile([P, CHANNELS], F32)
             for half in range(HALVES):
-                cols = slice(half * BANK, (half + 1) * BANK)
+                cols = half_cols(half)
                 nc.vector.tensor_tensor(out=q[:, cols], in0=q_banks[tile_no][half][:], in1=bq_all[:, cols], op=ALU.add)
             squares = work.tile([P, CHANNELS], BF16)
             sum_sq = small.tile([P, 1], F32)
             nc.scalar.activation(out=squares[:], in_=q[:], func=ACT.Square, accum_out=sum_sq[:])
-            norm = small.tile([P, 1], F32)
-            nc.scalar.activation(out=norm[:], in_=sum_sq[:], func=ACT.Sqrt)
-            q_of[tile_no] = (q, norm)
+            inv_norm = small.tile([P, 1], F32)
+            nc.gpsimd.tensor_tensor(out=inv_norm[:], in0=sum_sq[:], in1=minus_half[:], op=ALU.pow)
+            q_of[tile_no] = (q, inv_norm)
+
+        def weights(tile_no):
+            weight_ps = psum.tile([P, P], BF16, bufs=1)
+            nc.tensor.transpose(weight_ps[:], weight_cols[:, tile_no, :], ident_bf[:])
+            weight_rows = work.tile([P, P], BF16)
+            nc.scalar.copy(out=weight_rows[:], in_=weight_ps[:])
+            weight_rows_of[tile_no] = weight_rows
 
         def gate_mm(tile_no):
             image = tile_no // TILES_PER_IMAGE
             banks = []
             for half in range(HALVES):
-                cols = slice(half * BANK, (half + 1) * BANK)
                 gate_ps = psum.tile([P, BANK], F32)
                 nc.tensor.matmul(
-                    out=gate_ps[:], lhsT=weight_rows[:, tile_no, :], rhs=kv_rows[image][:, cols], start=True, stop=True
+                    out=gate_ps[:], lhsT=weight_rows_of[tile_no][:], rhs=kv_rows[image][:, half_cols(half)],
+                    start=True, stop=True,
                 )
                 banks.append(gate_ps)
             gate_banks[tile_no] = banks
 
         def gate_apply(tile_no):
-            q, norm = q_of[tile_no]
-            inv_norm = small.tile([P, 1], F32)
-            nc.vector.reciprocal(out=inv_norm[:], in_=norm[:])
+            q, inv_norm = q_of[tile_no]
             g_rows = work.tile([P, CHANNELS], BF16)
             for half in range(HALVES):
-                cols = slice(half * BANK, (half + 1) * BANK)
+                cols = half_cols(half)
                 nc.vector.scalar_tensor_tensor(
                     out=g_rows[:, cols], in0=q[:, cols], scalar=inv_norm[:, 0:1], in1=gate_banks[tile_no][half][:],
                     op0=ALU.mult, op1=ALU.mult,
@@ -242,7 +255,7 @@ def tile_hydraattention_pb_kernel(
         def turn(tile_no):
             pairs = g_rows_of[tile_no][:].bitcast(F32)
             pair_cols = K_PASS // 2
-            turned = psum.tile([P, GROUPS, 2, P], F32)
+            turned = psum.tile([P, GROUPS, 2, P], F32, bufs=1)
             for g in range(GROUPS):
                 for u in range(2):
                     nc.tensor.transpose(
@@ -265,27 +278,23 @@ def tile_hydraattention_pb_kernel(
             image, in_image = divmod(tile_no, TILES_PER_IMAGE)
             y = work.tile([P, CHANNELS], F32)
             for half in range(HALVES):
-                cols = slice(half * BANK, (half + 1) * BANK)
-                if tile_no % 2 == 0:
-                    nc.vector.tensor_tensor(out=y[:, cols], in0=y_banks[tile_no][half][:], in1=bo_all[:, cols], op=ALU.add)
-                else:
-                    nc.scalar.copy(out=y[:, cols], in_=y_banks[tile_no][half][:])
-                    nc.gpsimd.tensor_tensor(out=y[:, cols], in0=y[:, cols], in1=bo_all[:, cols], op=ALU.add)
-            nc.sync.dma_start(out=out[image, in_image * P : (in_image + 1) * P, :], in_=y[:])
+                cols = half_cols(half)
+                nc.vector.tensor_tensor(out=y[:, cols], in0=y_banks[tile_no][half][:], in1=bo_all[:, cols], op=ALU.add)
+                nc.sync.dma_start(out=out[image, in_image * P : (in_image + 1) * P, cols], in_=y[:, cols])
 
         def run(stage, tile_no):
             if 0 <= tile_no < TILES:
                 stage(tile_no)
 
-        with tc.manual_schedule():
-            for s in range(-4, TILES + 3):
-                run(outputs_exit, s - 3)
-                run(outputs_mm, s - 2)
-                run(queries_exit, s + 1)
-                run(queries_mm, s + 2)
-                run(gate_apply, s)
-                run(gate_mm, s + 1)
-                run(turn, s)
-                run(quantise_g, s - 1)
-                run(regroup_x, s + 4)
-                run(quantise_x, s + 3)
+        for s in range(-4, TILES + 3):
+            run(outputs_exit, s - 3)
+            run(outputs_mm, s - 2)
+            run(queries_exit, s + 1)
+            run(queries_mm, s + 2)
+            run(gate_apply, s)
+            run(gate_mm, s + 1)
+            run(turn, s)
+            run(weights, s + 2)
+            run(quantise_g, s - 1)
+            run(regroup_x, s + 4)
+            run(quantise_x, s + 3)

@@ -171,12 +171,12 @@ def tile_hydraattention_pb_kernel(
             image, in_image = divmod(tile_no, TILES_PER_IMAGE)
             chunk, in_chunk = divmod(in_image, TILES_PER_CHUNK)
             pixels = slice(in_chunk * P, (in_chunk + 1) * P)
-            copy = nc.vector.tensor_copy if tile_no < TILES_PER_CHUNK else nc.scalar.copy
             x_grouped = work.tile([P, GROUPS, P, PACK], BF16, align_bytes=64)
             for g in range(GROUPS):
-                copy(
-                    out=x_grouped[:, g].rearrange("p (c i) j -> p c j i", i=4),
-                    in_=x_raw[(image, chunk, g)][:, :, pixels].rearrange("p j (c i) -> p c j i", i=4),
+                nc.gpsimd.tensor_scalar(
+                    out=x_grouped[:, g],
+                    in0=x_raw[(image, chunk, g)][:, :, pixels].rearrange("p j w -> p w j"),
+                    scalar1=1.0, scalar2=0.0, op0=ALU.mult, op1=ALU.add,
                 )
             x_grouped_of[tile_no] = x_grouped
 
@@ -189,11 +189,11 @@ def tile_hydraattention_pb_kernel(
         def quantise_x(tile_no):
             x_mx[tile_no] = quantise(x_grouped_of[tile_no][:].rearrange("p g w j -> p (g w j)"), "x")
 
-        def project(operand, words, first_plane, tag):
+        def project(operand, words, first_plane):
             codes, scales = operand
             banks = []
             for half in range(HALVES):
-                acc = psum.tile([P, BANK], F32, tag=tag)
+                acc = psum.tile([P, BANK], F32, bufs=4)
                 for g in range(GROUPS):
                     nc.tensor.matmul_mx(
                         out=acc[:],
@@ -208,7 +208,7 @@ def tile_hydraattention_pb_kernel(
             return banks
 
         def queries_mm(tile_no):
-            q_banks[tile_no] = project(x_mx[tile_no], wq_words, 0, "q_ps")
+            q_banks[tile_no] = project(x_mx[tile_no], wq_words, 0)
 
         def queries_exit(tile_no):
             q = work.tile([P, CHANNELS], F32)
@@ -272,15 +272,18 @@ def tile_hydraattention_pb_kernel(
             g_mx[tile_no] = quantise(g_grouped_of[tile_no][:], "g")
 
         def outputs_mm(tile_no):
-            y_banks[tile_no] = project(g_mx[tile_no], wo_words, GROUPS, "y_ps")
+            y_banks[tile_no] = project(g_mx[tile_no], wo_words, GROUPS)
 
         def outputs_exit(tile_no):
             image, in_image = divmod(tile_no, TILES_PER_IMAGE)
+            rows = out[image, in_image * P : (in_image + 1) * P, :]
+            first, second = half_cols(0), half_cols(1)
             y = work.tile([P, CHANNELS], F32)
-            for half in range(HALVES):
-                cols = half_cols(half)
-                nc.vector.tensor_tensor(out=y[:, cols], in0=y_banks[tile_no][half][:], in1=bo_all[:, cols], op=ALU.add)
-                nc.sync.dma_start(out=out[image, in_image * P : (in_image + 1) * P, cols], in_=y[:, cols])
+            nc.vector.tensor_tensor(out=y[:, first], in0=y_banks[tile_no][0][:], in1=bo_all[:, first], op=ALU.add)
+            nc.sync.dma_start(out=rows[:, first], in_=y[:, first])
+            nc.scalar.copy(out=y[:, second], in_=y_banks[tile_no][1][:])
+            nc.gpsimd.tensor_tensor(out=y[:, second], in0=y[:, second], in1=bo_all[:, second], op=ALU.add)
+            nc.sync.dma_start(out=rows[:, second], in_=y[:, second])
 
         def run(stage, tile_no):
             if 0 <= tile_no < TILES:
@@ -289,6 +292,7 @@ def tile_hydraattention_pb_kernel(
         for s in range(-4, TILES + 3):
             run(outputs_exit, s - 3)
             run(outputs_mm, s - 2)
+            run(regroup_x, s + 4)
             run(queries_exit, s + 1)
             run(queries_mm, s + 2)
             run(gate_apply, s)
@@ -296,5 +300,4 @@ def tile_hydraattention_pb_kernel(
             run(turn, s)
             run(weights, s + 2)
             run(quantise_g, s - 1)
-            run(regroup_x, s + 4)
             run(quantise_x, s + 3)

@@ -47,16 +47,22 @@ def tile_hydraattention_pb_kernel(
         psum = ctx.enter_context(tc.psum_pool(name="psum", bufs=2))
         ctx.enter_context(tc.manual_schedule())
 
+        minus_half = keep.tile([P, 1], F32)
+        nc.vector.memset(minus_half[:], -0.5)
+        warm = keep.tile([P, 1], F32)
+        nc.scalar.activation(out=warm[:], in_=minus_half[:], func=ACT.Square)
+
 
         mask_rows = keep.tile([P, P], BF16)
-        nc.vector.memset(mask_rows[:], 0.0)
+        nc.vector.memset(mask_rows[:].bitcast(I32), 0)
         nc.sync.dma_start(
             out=mask_rows[0:TILES, :],
             in_=mask.rearrange("b o (i r) w -> (b o i) (r w)", i=TILES_PER_IMAGE),
         )
-        bq_row = keep.tile([P, CHANNELS], BF16)
-        nc.vector.memset(bq_row[:], 0.0)
-        nc.sync.dma_start(out=bq_row[0:1, :], in_=b_q.unsqueeze(0))
+        bias_rows = keep.tile([P, CHANNELS], BF16)
+        nc.vector.memset(bias_rows[:].bitcast(I32), 0)
+        nc.sync.dma_start(out=bias_rows[0:1, :], in_=b_q.unsqueeze(0))
+        nc.sync.dma_start(out=bias_rows[1:2, :], in_=b_out.unsqueeze(0))
 
         x_raw = {}
 
@@ -67,60 +73,52 @@ def tile_hydraattention_pb_kernel(
                 nc.sync.dma_start(out=raw[:], in_=rows[:, :, chunk * CHUNK : (chunk + 1) * CHUNK])
                 x_raw[(image, chunk, g)] = raw
 
-        planes = keep.tile([P, CHANNELS], U8, align_bytes=64)
-        nc.vector.memset(planes[:].bitcast(I32), 0)
+        def load_weight(words_in, scales_in, name):
+            words = keep.tile([P, GROUPS, CHANNELS], U32, name=name + "_words", align_bytes=64)
+            planes = keep.tile([P, CHANNELS], U8, name=name + "_planes", align_bytes=64)
+            nc.vector.memset(planes[:].bitcast(I32), 0)
 
-        def load_weight(words_in, scales_in, first_plane, name):
-            for quadrant in range(4):
-                top = 32 * quadrant + PLANE_ROWS * first_plane
-                nc.sync.dma_start(
-                    out=planes[top : top + GROUPS * PLANE_ROWS, :].bitcast(I32),
-                    in_=scales_in[:, PLANE_ROWS * quadrant : PLANE_ROWS * (quadrant + 1), :].bitcast(I32),
-                )
-            words = keep.tile([P, GROUPS, CHANNELS], U32, name=name, align_bytes=64)
-            for half in range(HALVES):
+            def load_words(half):
                 for g in range(GROUPS):
                     nc.sync.dma_start(
                         out=words[:, g, half_cols(half)].bitcast(I32),
                         in_=words_in[g, :, half_cols(half), :].rearrange("p n t -> p (n t)").bitcast(I32),
                     )
-            return words
 
-        def scale_plane(number, cols):
-            return planes[PLANE_ROWS * number : P, cols]
-
-        load_x(0, 0)
-        wq_words = load_weight(W_q_words, W_q_scales, 0, "wq_words")
-        load_x(0, 1)
-        wo_words = load_weight(W_out_words, W_out_scales, GROUPS, "wo_words")
-        for chunk in range(2, CHUNKS):
-            load_x(0, chunk)
-        for chunk in range(CHUNKS):
-            load_x(1, chunk)
-
-        bo_row = keep.tile([P, CHANNELS], BF16)
-        nc.vector.memset(bo_row[:], 0.0)
-        nc.scalar.dma_start(out=bo_row[0:1, :], in_=b_out.unsqueeze(0))
-        kv_rows = []
-        for image in range(IMAGES):
-            rows = keep.tile([P, CHANNELS], BF16, name="kv_rows_%d" % image)
-            nc.vector.memset(rows[:], 0.0)
-            nc.scalar.dma_start(out=rows[0:PIECES, :], in_=kv_know[image, 0].partition_broadcast(PIECES))
-            nc.scalar.dma_start(out=rows[PIECES : 2 * PIECES, :], in_=kv_mask[image, 0].partition_broadcast(PIECES))
-            kv_rows.append(rows)
+            load_words(0)
+            for quadrant in range(4):
+                nc.sync.dma_start(
+                    out=planes[32 * quadrant : 32 * quadrant + GROUPS * PLANE_ROWS, :].bitcast(I32),
+                    in_=scales_in[:, PLANE_ROWS * quadrant : PLANE_ROWS * (quadrant + 1), :].bitcast(I32),
+                )
+            load_words(1)
+            return words, planes
 
         ident_bf = keep.tile([P, P], BF16)
         make_identity(nc, ident_bf[:])
+        weight_cols = keep.tile([P, TILES, P], BF16)
+        nc.vector.memset(weight_cols[:].bitcast(I32), 0)
+
+        def load_kv(image):
+            rows = keep.tile([P, CHANNELS], BF16, name="kv_rows_%d" % image)
+            nc.gpsimd.memset(rows[:], 0.0)
+            nc.sync.dma_start(out=rows[0:PIECES, :], in_=kv_know[image, 0].partition_broadcast(PIECES))
+            nc.sync.dma_start(out=rows[PIECES : 2 * PIECES, :], in_=kv_mask[image, 0].partition_broadcast(PIECES))
+            return rows
+
+        load_x(0, 0)
+        w_q = load_weight(W_q_words, W_q_scales, "wq")
+        kv_rows = [load_kv(0)]
+        load_x(0, 1)
+        load_x(0, 2)
+        w_out = load_weight(W_out_words, W_out_scales, "wo")
+        load_x(0, 3)
+        kv_rows.append(load_kv(1))
+        for chunk in range(CHUNKS):
+            load_x(1, chunk)
+
         ident_f32 = keep.tile([P, P], F32)
         make_identity(nc, ident_f32[:])
-        ones = keep.tile([P, P], BF16)
-        nc.vector.memset(ones[:], 1.0)
-        minus_half = keep.tile([P, 1], F32)
-        nc.vector.memset(minus_half[:], -0.5)
-        weight_cols = keep.tile([P, TILES, P], BF16)
-        nc.vector.memset(weight_cols[:], 0.0)
-        warm = keep.tile([P, 1], F32)
-        nc.scalar.activation(out=warm[:], in_=minus_half[:], func=ACT.Square)
 
         mask_ps = psum.tile([P, P], BF16, tag="weight_ps", bufs=1)
         nc.tensor.transpose(mask_ps[:], mask_rows[:], ident_bf[:])
@@ -130,31 +128,30 @@ def tile_hydraattention_pb_kernel(
         nc.vector.tensor_scalar(out=inv[:], in0=m[:], scalar1=-1.0, scalar2=1.0, op0=ALU.mult, op1=ALU.add)
         blend = keep.tile([P, TILES], F32)
         nc.vector.scalar_tensor_tensor(out=blend[:], in0=m[:], scalar=0.3, in1=inv[:], op0=ALU.mult, op1=ALU.add)
-        know_w = keep.tile([P, TILES], F32)
-        nc.vector.tensor_tensor(out=know_w[:], in0=inv[:], in1=blend[:], op=ALU.mult)
-        mask_w = keep.tile([P, TILES], F32)
-        nc.vector.scalar_tensor_tensor(out=mask_w[:], in0=m[:], scalar=0.7, in1=m[:], op0=ALU.mult, op1=ALU.mult)
+        gate_w = keep.tile([P, TILES, 2], F32)
+        nc.vector.tensor_tensor(out=gate_w[:, :, 0], in0=inv[:], in1=blend[:], op=ALU.mult)
+        nc.vector.scalar_tensor_tensor(out=gate_w[:, :, 1], in0=m[:], scalar=0.7, in1=m[:], op0=ALU.mult, op1=ALU.mult)
 
-        for first_row, weight in ((0, know_w), (PIECES, mask_w)):
-            rest = weight
-            for piece in range(PIECES):
-                column = weight_cols[:, :, first_row + piece]
-                nc.vector.tensor_copy(out=column, in_=rest[:])
-                if piece < PIECES - 1:
-                    smaller = keep.tile([P, TILES], F32, name="rest_%d_%d" % (first_row, piece))
-                    nc.vector.tensor_tensor(out=smaller[:], in0=rest[:], in1=column, op=ALU.subtract)
-                    rest = smaller
+        rest = gate_w
+        for piece in range(PIECES):
+            columns = weight_cols[:, :, piece : 2 * PIECES : PIECES]
+            nc.vector.tensor_copy(out=columns, in_=rest[:])
+            if piece < PIECES - 1:
+                smaller = keep.tile([P, TILES, 2], F32, name="rest_%d" % piece)
+                nc.vector.tensor_tensor(out=smaller[:], in0=rest[:], in1=columns, op=ALU.subtract)
+                rest = smaller
 
-        def spread(bias_row, name):
+        def spread(row, name):
             bias_all = keep.tile([P, CHANNELS], BF16, name=name)
+            pick = ident_bf[:, row : row + 1].to_broadcast([P, P])
             for half in range(HALVES):
                 bias_ps = psum.tile([P, BANK], F32, tag="gate_ps")
-                nc.tensor.matmul(out=bias_ps[:], lhsT=ones[:], rhs=bias_row[:, half_cols(half)], start=True, stop=True)
+                nc.tensor.matmul(out=bias_ps[:], lhsT=pick, rhs=bias_rows[:, half_cols(half)], start=True, stop=True)
                 nc.scalar.copy(out=bias_all[:, half_cols(half)], in_=bias_ps[:])
             return bias_all
 
-        bq_all = spread(bq_row, "bq_all")
-        bo_all = spread(bo_row, "bo_all")
+        bq_all = spread(0, "bq_all")
+        bo_all = spread(1, "bo_all")
 
         x_grouped_of = {}
         x_mx = {}
@@ -171,12 +168,12 @@ def tile_hydraattention_pb_kernel(
             image, in_image = divmod(tile_no, TILES_PER_IMAGE)
             chunk, in_chunk = divmod(in_image, TILES_PER_CHUNK)
             pixels = slice(in_chunk * P, (in_chunk + 1) * P)
+            copy = nc.vector.tensor_copy if tile_no < TILES_PER_CHUNK else nc.scalar.copy
             x_grouped = work.tile([P, GROUPS, P, PACK], BF16, align_bytes=64)
             for g in range(GROUPS):
-                nc.gpsimd.tensor_scalar(
-                    out=x_grouped[:, g],
-                    in0=x_raw[(image, chunk, g)][:, :, pixels].rearrange("p j w -> p w j"),
-                    scalar1=1.0, scalar2=0.0, op0=ALU.mult, op1=ALU.add,
+                copy(
+                    out=x_grouped[:, g].rearrange("p (c i) j -> p c j i", i=4),
+                    in_=x_raw[(image, chunk, g)][:, :, pixels].rearrange("p j (c i) -> p c j i", i=4),
                 )
             x_grouped_of[tile_no] = x_grouped
 
@@ -189,8 +186,9 @@ def tile_hydraattention_pb_kernel(
         def quantise_x(tile_no):
             x_mx[tile_no] = quantise(x_grouped_of[tile_no][:].rearrange("p g w j -> p (g w j)"), "x")
 
-        def project(operand, words, first_plane):
+        def project(operand, weight):
             codes, scales = operand
+            words, planes = weight
             banks = []
             for half in range(HALVES):
                 acc = psum.tile([P, BANK], F32, bufs=4)
@@ -200,7 +198,7 @@ def tile_hydraattention_pb_kernel(
                         lhsT=codes[:, g * P : (g + 1) * P].bitcast(FP8X4),
                         lhsT_scale=scales[:, g * P : (g + 1) * P],
                         rhs=words[:, g, half_cols(half)].bitcast(FP8X4),
-                        rhs_scale=scale_plane(first_plane + g, half_cols(half)),
+                        rhs_scale=planes[PLANE_ROWS * g : P, half_cols(half)],
                         start=(g == 0),
                         stop=(g == GROUPS - 1),
                     )
@@ -208,7 +206,7 @@ def tile_hydraattention_pb_kernel(
             return banks
 
         def queries_mm(tile_no):
-            q_banks[tile_no] = project(x_mx[tile_no], wq_words, 0)
+            q_banks[tile_no] = project(x_mx[tile_no], w_q)
 
         def queries_exit(tile_no):
             q = work.tile([P, CHANNELS], F32)
@@ -272,18 +270,15 @@ def tile_hydraattention_pb_kernel(
             g_mx[tile_no] = quantise(g_grouped_of[tile_no][:], "g")
 
         def outputs_mm(tile_no):
-            y_banks[tile_no] = project(g_mx[tile_no], wo_words, GROUPS)
+            y_banks[tile_no] = project(g_mx[tile_no], w_out)
 
         def outputs_exit(tile_no):
             image, in_image = divmod(tile_no, TILES_PER_IMAGE)
-            rows = out[image, in_image * P : (in_image + 1) * P, :]
-            first, second = half_cols(0), half_cols(1)
             y = work.tile([P, CHANNELS], F32)
-            nc.vector.tensor_tensor(out=y[:, first], in0=y_banks[tile_no][0][:], in1=bo_all[:, first], op=ALU.add)
-            nc.sync.dma_start(out=rows[:, first], in_=y[:, first])
-            nc.scalar.copy(out=y[:, second], in_=y_banks[tile_no][1][:])
-            nc.gpsimd.tensor_tensor(out=y[:, second], in0=y[:, second], in1=bo_all[:, second], op=ALU.add)
-            nc.sync.dma_start(out=rows[:, second], in_=y[:, second])
+            for half in range(HALVES):
+                cols = half_cols(half)
+                nc.vector.tensor_tensor(out=y[:, cols], in0=y_banks[tile_no][half][:], in1=bo_all[:, cols], op=ALU.add)
+                nc.sync.dma_start(out=out[image, in_image * P : (in_image + 1) * P, cols], in_=y[:, cols])
 
         def run(stage, tile_no):
             if 0 <= tile_no < TILES:
@@ -292,7 +287,6 @@ def tile_hydraattention_pb_kernel(
         for s in range(-4, TILES + 3):
             run(outputs_exit, s - 3)
             run(outputs_mm, s - 2)
-            run(regroup_x, s + 4)
             run(queries_exit, s + 1)
             run(queries_mm, s + 2)
             run(gate_apply, s)
@@ -301,3 +295,4 @@ def tile_hydraattention_pb_kernel(
             run(weights, s + 2)
             run(quantise_g, s - 1)
             run(quantise_x, s + 3)
+            run(regroup_x, s + 4)

@@ -274,11 +274,14 @@ def tile_hydraattention_pb_kernel(
 
         def outputs_exit(tile_no):
             image, in_image = divmod(tile_no, TILES_PER_IMAGE)
+            rows = out[image, in_image * P : (in_image + 1) * P, :]
+            first, second = half_cols(0), half_cols(1)
             y = work.tile([P, CHANNELS], F32)
-            for half in range(HALVES):
-                cols = half_cols(half)
-                nc.vector.tensor_tensor(out=y[:, cols], in0=y_banks[tile_no][half][:], in1=bo_all[:, cols], op=ALU.add)
-                nc.sync.dma_start(out=out[image, in_image * P : (in_image + 1) * P, cols], in_=y[:, cols])
+            nc.vector.tensor_tensor(out=y[:, first], in0=y_banks[tile_no][0][:], in1=bo_all[:, first], op=ALU.add)
+            nc.sync.dma_start(out=rows[:, first], in_=y[:, first])
+            nc.scalar.copy(out=y[:, second], in_=y_banks[tile_no][1][:])
+            nc.gpsimd.tensor_tensor(out=y[:, second], in0=y[:, second], in1=bo_all[:, second], op=ALU.add)
+            nc.sync.dma_start(out=rows[:, second], in_=y[:, second])
 
         def run(stage, tile_no):
             if 0 <= tile_no < TILES:
@@ -288,6 +291,7 @@ def tile_hydraattention_pb_kernel(
             run(outputs_exit, s - 3)
             run(outputs_mm, s - 2)
             run(queries_exit, s + 1)
+            run(regroup_x, s + 4)
             run(queries_mm, s + 2)
             run(gate_apply, s)
             run(gate_mm, s + 1)
@@ -295,4 +299,3 @@ def tile_hydraattention_pb_kernel(
             run(weights, s + 2)
             run(quantise_g, s - 1)
             run(quantise_x, s + 3)
-            run(regroup_x, s + 4)

@@ -287,14 +287,14 @@ def tile_hydraattention_pb_kernel(
             if 0 <= tile_no < TILES:
                 stage(tile_no)
 
-        for s in range(-4, TILES + 3):
-            run(outputs_exit, s - 3)
+        for s in range(-4, TILES + 2):
             run(outputs_mm, s - 2)
             run(queries_exit, s + 1)
             run(regroup_x, s + 4)
             run(queries_mm, s + 2)
             run(gate_apply, s)
             run(gate_mm, s + 1)
+            run(outputs_exit, s - 2)
             run(turn, s)
             run(weights, s + 2)
             run(quantise_g, s - 1)

@@ -28,6 +28,10 @@ CHUNKS = PIXELS // CHUNK
 TILES_PER_CHUNK = CHUNK // P
 PIECES = 3
 PLANE_ROWS = 4
+KINDS = 2 * IMAGES
+ROWS_PER_KIND = PIECES * TILES_PER_IMAGE
+GATE_ROWS = KINDS * ROWS_PER_KIND
+FIRST_STEP = -2
 
 FLOPS = 2 * 2 * IMAGES * PIXELS * CHANNELS * CHANNELS
 
@@ -53,6 +57,31 @@ def tile_hydraattention_pb_kernel(
         nc.scalar.activation(out=warm[:], in_=minus_half[:], func=ACT.Square)
 
 
+        def weight_tiles(name):
+            words = keep.tile([P, GROUPS, CHANNELS], U32, name=name + "_words", align_bytes=64)
+            planes = keep.tile([P, CHANNELS], U8, name=name + "_planes", align_bytes=64)
+            nc.vector.memset(planes[:].bitcast(I32), 0)
+            return words, planes
+
+        def load_planes(weight, scales_in):
+            planes = weight[1]
+            for quadrant in range(4):
+                nc.sync.dma_start(
+                    out=planes[32 * quadrant : 32 * quadrant + GROUPS * PLANE_ROWS, :].bitcast(I32),
+                    in_=scales_in[:, PLANE_ROWS * quadrant : PLANE_ROWS * (quadrant + 1), :].bitcast(I32),
+                )
+
+        def load_words(weight, words_in, half):
+            words = weight[0]
+            for g in range(GROUPS):
+                nc.sync.dma_start(
+                    out=words[:, g, half_cols(half)].bitcast(I32),
+                    in_=words_in[g, :, half_cols(half), :].rearrange("p n t -> p (n t)").bitcast(I32),
+                )
+
+        w_q = weight_tiles("wq")
+        load_planes(w_q, W_q_scales)
+
         mask_rows = keep.tile([P, P], BF16)
         nc.vector.memset(mask_rows[:].bitcast(I32), 0)
         nc.sync.dma_start(
@@ -73,73 +102,75 @@ def tile_hydraattention_pb_kernel(
                 nc.sync.dma_start(out=raw[:], in_=rows[:, :, chunk * CHUNK : (chunk + 1) * CHUNK])
                 x_raw[(image, chunk, g)] = raw
 
-        def load_weight(words_in, scales_in, name):
-            words = keep.tile([P, GROUPS, CHANNELS], U32, name=name + "_words", align_bytes=64)
-            planes = keep.tile([P, CHANNELS], U8, name=name + "_planes", align_bytes=64)
-            nc.vector.memset(planes[:].bitcast(I32), 0)
-
-            def load_words(half):
-                for g in range(GROUPS):
-                    nc.sync.dma_start(
-                        out=words[:, g, half_cols(half)].bitcast(I32),
-                        in_=words_in[g, :, half_cols(half), :].rearrange("p n t -> p (n t)").bitcast(I32),
-                    )
-
-            load_words(0)
-            for quadrant in range(4):
-                nc.sync.dma_start(
-                    out=planes[32 * quadrant : 32 * quadrant + GROUPS * PLANE_ROWS, :].bitcast(I32),
-                    in_=scales_in[:, PLANE_ROWS * quadrant : PLANE_ROWS * (quadrant + 1), :].bitcast(I32),
-                )
-            load_words(1)
-            return words, planes
-
         ident_bf = keep.tile([P, P], BF16)
         make_identity(nc, ident_bf[:])
-        weight_cols = keep.tile([P, TILES, P], BF16)
+        weight_cols = keep.tile([P, P], BF16)
         nc.vector.memset(weight_cols[:].bitcast(I32), 0)
 
+        kv_rows = keep.tile([P, CHANNELS], BF16)
+        nc.gpsimd.memset(kv_rows[:], 0.0)
+
         def load_kv(image):
-            rows = keep.tile([P, CHANNELS], BF16, name="kv_rows_%d" % image)
-            nc.gpsimd.memset(rows[:], 0.0)
-            nc.sync.dma_start(out=rows[0:PIECES, :], in_=kv_know[image, 0].partition_broadcast(PIECES))
-            nc.sync.dma_start(out=rows[PIECES : 2 * PIECES, :], in_=kv_mask[image, 0].partition_broadcast(PIECES))
-            return rows
+            for which, vector in enumerate((kv_know, kv_mask)):
+                first = (2 * image + which) * ROWS_PER_KIND
+                nc.sync.dma_start(
+                    out=kv_rows[first : first + ROWS_PER_KIND, :], in_=vector[image, 0].partition_broadcast(ROWS_PER_KIND)
+                )
 
         load_x(0, 0)
-        w_q = load_weight(W_q_words, W_q_scales, "wq")
-        kv_rows = [load_kv(0)]
+        load_words(w_q, W_q_words, 0)
+        load_words(w_q, W_q_words, 1)
         load_x(0, 1)
+        load_kv(0)
+        load_kv(1)
         load_x(0, 2)
-        w_out = load_weight(W_out_words, W_out_scales, "wo")
+        w_out = weight_tiles("wo")
+        load_words(w_out, W_out_words, 0)
+        load_planes(w_out, W_out_scales)
+        load_words(w_out, W_out_words, 1)
         load_x(0, 3)
-        kv_rows.append(load_kv(1))
         for chunk in range(CHUNKS):
             load_x(1, chunk)
 
         ident_f32 = keep.tile([P, P], F32)
         make_identity(nc, ident_f32[:])
 
-        mask_ps = psum.tile([P, P], BF16, tag="weight_ps", bufs=1)
-        nc.tensor.transpose(mask_ps[:], mask_rows[:], ident_bf[:])
+        mask_ps = psum.tile([P, 2 * BANK], BF16, tag="turned")
+        nc.tensor.transpose(mask_ps[:, 0:P], mask_rows[:], ident_bf[:])
         m = keep.tile([P, TILES], F32)
         nc.vector.tensor_copy(out=m[:], in_=mask_ps[:, 0:TILES])
         inv = keep.tile([P, TILES], F32)
         nc.vector.tensor_scalar(out=inv[:], in0=m[:], scalar1=-1.0, scalar2=1.0, op0=ALU.mult, op1=ALU.add)
         blend = keep.tile([P, TILES], F32)
         nc.vector.scalar_tensor_tensor(out=blend[:], in0=m[:], scalar=0.3, in1=inv[:], op0=ALU.mult, op1=ALU.add)
-        gate_w = keep.tile([P, TILES, 2], F32)
-        nc.vector.tensor_tensor(out=gate_w[:, :, 0], in0=inv[:], in1=blend[:], op=ALU.mult)
-        nc.vector.scalar_tensor_tensor(out=gate_w[:, :, 1], in0=m[:], scalar=0.7, in1=m[:], op0=ALU.mult, op1=ALU.mult)
+        def by_image(ap):
+            return ap.rearrange("p (b i) -> p b i", b=IMAGES)
 
-        rest = gate_w
-        for piece in range(PIECES):
-            columns = weight_cols[:, :, piece : 2 * PIECES : PIECES]
-            nc.vector.tensor_copy(out=columns, in_=rest[:])
-            if piece < PIECES - 1:
-                smaller = keep.tile([P, TILES, 2], F32, name="rest_%d" % piece)
-                nc.vector.tensor_tensor(out=smaller[:], in0=rest[:], in1=columns, op=ALU.subtract)
-                rest = smaller
+        gate_w = keep.tile([P, KINDS, TILES_PER_IMAGE], F32)
+        nc.vector.tensor_tensor(out=gate_w[:, 0:KINDS:2, :], in0=by_image(inv[:]), in1=by_image(blend[:]), op=ALU.mult)
+        nc.vector.scalar_tensor_tensor(
+            out=gate_w[:, 1:KINDS:2, :], in0=by_image(m[:]), scalar=0.7, in1=by_image(m[:]), op0=ALU.mult, op1=ALU.mult
+        )
+        tile_rows = keep.tile([P, TILES], F32)
+        nc.vector.tensor_reduce(
+            out=by_image(tile_rows[:]),
+            in_=ident_bf[:, 0:GATE_ROWS].rearrange("p (b k i) -> p b i k", b=IMAGES, i=TILES_PER_IMAGE),
+            axis=mybir.AxisListType.X, op=ALU.add,
+        )
+
+        rests = [gate_w]
+
+        def piece_columns(piece):
+            by_kind = weight_cols[:, 0:GATE_ROWS].rearrange("p (k c i) -> p k c i", k=KINDS, c=PIECES)
+            return by_kind[:, :, piece, :]
+
+        def cut_piece(piece):
+            nc.vector.tensor_copy(out=piece_columns(piece), in_=rests[piece][:])
+
+        def take_rest(piece):
+            smaller = keep.tile([P, KINDS, TILES_PER_IMAGE], F32, name="rest_%d" % piece)
+            nc.vector.tensor_tensor(out=smaller[:], in0=rests[piece][:], in1=piece_columns(piece), op=ALU.subtract)
+            rests.append(smaller)
 
         def spread(row, name):
             bias_all = keep.tile([P, CHANNELS], BF16, name=name)
@@ -220,20 +251,27 @@ def tile_hydraattention_pb_kernel(
             nc.gpsimd.tensor_tensor(out=inv_norm[:], in0=sum_sq[:], in1=minus_half[:], op=ALU.pow)
             q_of[tile_no] = (q, inv_norm)
 
+        all_weight_rows = keep.tile([P, P], BF16)
+
+        def turn_weights():
+            weight_ps = psum.tile([P, 2 * BANK], BF16, tag="turned")
+            nc.tensor.transpose(weight_ps[:, 0:P], weight_cols[:], ident_bf[:])
+            nc.scalar.copy(out=all_weight_rows[:], in_=weight_ps[:, 0:P])
+
         def weights(tile_no):
-            weight_ps = psum.tile([P, P], BF16, bufs=1)
-            nc.tensor.transpose(weight_ps[:], weight_cols[:, tile_no, :], ident_bf[:])
             weight_rows = work.tile([P, P], BF16)
-            nc.scalar.copy(out=weight_rows[:], in_=weight_ps[:])
+            nc.gpsimd.tensor_scalar(
+                out=weight_rows[:], in0=all_weight_rows[:], scalar1=tile_rows[:, tile_no : tile_no + 1], scalar2=0.0,
+                op0=ALU.mult, op1=ALU.add,
+            )
             weight_rows_of[tile_no] = weight_rows
 
         def gate_mm(tile_no):
-            image = tile_no // TILES_PER_IMAGE
             banks = []
             for half in range(HALVES):
                 gate_ps = psum.tile([P, BANK], F32)
                 nc.tensor.matmul(
-                    out=gate_ps[:], lhsT=weight_rows_of[tile_no][:], rhs=kv_rows[image][:, half_cols(half)],
+                    out=gate_ps[:], lhsT=weight_rows_of[tile_no][:], rhs=kv_rows[:, half_cols(half)],
                     start=True, stop=True,
                 )
                 banks.append(gate_ps)
@@ -253,7 +291,7 @@ def tile_hydraattention_pb_kernel(
         def turn(tile_no):
             pairs = g_rows_of[tile_no][:].bitcast(F32)
             pair_cols = K_PASS // 2
-            turned = psum.tile([P, GROUPS, 2, P], F32, bufs=1)
+            turned = psum.tile([P, GROUPS, 2, P], F32)
             for g in range(GROUPS):
                 for u in range(2):
                     nc.tensor.transpose(
@@ -279,23 +317,38 @@ def tile_hydraattention_pb_kernel(
             y = work.tile([P, CHANNELS], F32)
             nc.vector.tensor_tensor(out=y[:, first], in0=y_banks[tile_no][0][:], in1=bo_all[:, first], op=ALU.add)
             nc.sync.dma_start(out=rows[:, first], in_=y[:, first])
-            nc.scalar.copy(out=y[:, second], in_=y_banks[tile_no][1][:])
-            nc.gpsimd.tensor_tensor(out=y[:, second], in0=y[:, second], in1=bo_all[:, second], op=ALU.add)
+            if tile_no == TILES - 1:
+                nc.vector.tensor_tensor(out=y[:, second], in0=y_banks[tile_no][1][:], in1=bo_all[:, second], op=ALU.add)
+            else:
+                nc.scalar.copy(out=y[:, second], in_=y_banks[tile_no][1][:])
+                nc.gpsimd.tensor_tensor(out=y[:, second], in0=y[:, second], in1=bo_all[:, second], op=ALU.add)
             nc.sync.dma_start(out=rows[:, second], in_=y[:, second])
 
-        def run(stage, tile_no):
-            if 0 <= tile_no < TILES:
+        def run(stage, tile_no, first=0):
+            if first <= tile_no < TILES:
                 stage(tile_no)
 
-        for s in range(-4, TILES + 2):
+        regroup_x(0)
+        cut_piece(0)
+        quantise_x(0)
+        regroup_x(1)
+        take_rest(0)
+        quantise_x(1)
+        cut_piece(1)
+        take_rest(1)
+        cut_piece(2)
+
+        for s in range(FIRST_STEP, TILES + 2):
             run(outputs_mm, s - 2)
             run(queries_exit, s + 1)
             run(regroup_x, s + 4)
             run(queries_mm, s + 2)
             run(gate_apply, s)
             run(gate_mm, s + 1)
+            run(quantise_g, s - 1)
             run(outputs_exit, s - 2)
             run(turn, s)
+            if s == FIRST_STEP:
+                turn_weights()
             run(weights, s + 2)
-            run(quantise_g, s - 1)
-            run(quantise_x, s + 3)
+            run(quantise_x, s + 3, first=TILES_PER_CHUNK)

@@ -72,26 +72,10 @@ def tile_hydraattention_pb_kernel(
                 )
 
         def load_words(weight, words_in, half):
-            words = weight[0]
-            for g in range(GROUPS):
-                nc.sync.dma_start(
-                    out=words[:, g, half_cols(half)].bitcast(I32),
-                    in_=words_in[g, :, half_cols(half), :].rearrange("p n t -> p (n t)").bitcast(I32),
-                )
-
-        w_q = weight_tiles("wq")
-        load_planes(w_q, W_q_scales)
-
-        mask_rows = keep.tile([P, P], BF16)
-        nc.vector.memset(mask_rows[:].bitcast(I32), 0)
-        nc.sync.dma_start(
-            out=mask_rows[0:TILES, :],
-            in_=mask.rearrange("b o (i r) w -> (b o i) (r w)", i=TILES_PER_IMAGE),
-        )
-        bias_rows = keep.tile([P, CHANNELS], BF16)
-        nc.vector.memset(bias_rows[:].bitcast(I32), 0)
-        nc.sync.dma_start(out=bias_rows[0:1, :], in_=b_q.unsqueeze(0))
-        nc.sync.dma_start(out=bias_rows[1:2, :], in_=b_out.unsqueeze(0))
+            nc.sync.dma_start(
+                out=weight[0][:, :, half_cols(half)].bitcast(I32),
+                in_=words_in[:, :, half_cols(half), :].rearrange("g p n t -> p g (n t)").bitcast(I32),
+            )
 
         x_raw = {}
 
@@ -101,6 +85,22 @@ def tile_hydraattention_pb_kernel(
                 rows = x[image, g * K_PASS : (g + 1) * K_PASS].rearrange("(p j) r w -> p j (r w)", j=PACK)
                 nc.sync.dma_start(out=raw[:], in_=rows[:, :, chunk * CHUNK : (chunk + 1) * CHUNK])
                 x_raw[(image, chunk, g)] = raw
+
+        load_x(0, 0)
+        bias_rows = keep.tile([P, CHANNELS], BF16)
+        nc.vector.memset(bias_rows[:].bitcast(I32), 0)
+        nc.sync.dma_start(out=bias_rows[0:1, :], in_=b_q.unsqueeze(0))
+        nc.sync.dma_start(out=bias_rows[1:2, :], in_=b_out.unsqueeze(0))
+        mask_rows = keep.tile([P, P], BF16)
+        nc.vector.memset(mask_rows[:].bitcast(I32), 0)
+        nc.sync.dma_start(
+            out=mask_rows[0:TILES, :],
+            in_=mask.rearrange("b o (i r) w -> (b o i) (r w)", i=TILES_PER_IMAGE),
+        )
+        w_q = weight_tiles("wq")
+        load_words(w_q, W_q_words, 0)
+        load_planes(w_q, W_q_scales)
+        load_words(w_q, W_q_words, 1)
 
         ident_bf = keep.tile([P, P], BF16)
         make_identity(nc, ident_bf[:])
@@ -117,9 +117,6 @@ def tile_hydraattention_pb_kernel(
                     out=kv_rows[first : first + ROWS_PER_KIND, :], in_=vector[image, 0].partition_broadcast(ROWS_PER_KIND)
                 )
 
-        load_x(0, 0)
-        load_words(w_q, W_q_words, 0)
-        load_words(w_q, W_q_words, 1)
         load_x(0, 1)
         load_kv(0)
         load_kv(1)
@@ -138,19 +135,11 @@ def tile_hydraattention_pb_kernel(
         mask_ps = psum.tile([P, 2 * BANK], BF16, tag="turned")
         nc.tensor.transpose(mask_ps[:, 0:P], mask_rows[:], ident_bf[:])
         m = keep.tile([P, TILES], F32)
-        nc.vector.tensor_copy(out=m[:], in_=mask_ps[:, 0:TILES])
-        inv = keep.tile([P, TILES], F32)
-        nc.vector.tensor_scalar(out=inv[:], in0=m[:], scalar1=-1.0, scalar2=1.0, op0=ALU.mult, op1=ALU.add)
-        blend = keep.tile([P, TILES], F32)
-        nc.vector.scalar_tensor_tensor(out=blend[:], in0=m[:], scalar=0.3, in1=inv[:], op0=ALU.mult, op1=ALU.add)
+        nc.scalar.copy(out=m[:], in_=mask_ps[:, 0:TILES])
+
         def by_image(ap):
             return ap.rearrange("p (b i) -> p b i", b=IMAGES)
 
-        gate_w = keep.tile([P, KINDS, TILES_PER_IMAGE], F32)
-        nc.vector.tensor_tensor(out=gate_w[:, 0:KINDS:2, :], in0=by_image(inv[:]), in1=by_image(blend[:]), op=ALU.mult)
-        nc.vector.scalar_tensor_tensor(
-            out=gate_w[:, 1:KINDS:2, :], in0=by_image(m[:]), scalar=0.7, in1=by_image(m[:]), op0=ALU.mult, op1=ALU.mult
-        )
         tile_rows = keep.tile([P, TILES], F32)
         nc.vector.tensor_reduce(
             out=by_image(tile_rows[:]),
@@ -158,19 +147,25 @@ def tile_hydraattention_pb_kernel(
             axis=mybir.AxisListType.X, op=ALU.add,
         )
 
-        rests = [gate_w]
+        inv = keep.tile([P, TILES], F32)
+        nc.gpsimd.tensor_scalar(out=inv[:], in0=m[:], scalar1=-1.0, scalar2=1.0, op0=ALU.mult, op1=ALU.add)
+        blend = keep.tile([P, TILES], F32)
+        nc.gpsimd.tensor_scalar(out=blend[:], in0=m[:], scalar1=-0.7, scalar2=1.0, op0=ALU.mult, op1=ALU.add)
+        scaled = keep.tile([P, TILES], F32)
+        nc.gpsimd.tensor_scalar(out=scaled[:], in0=m[:], scalar1=0.7, scalar2=0.0, op0=ALU.mult, op1=ALU.add)
+        gate_w = keep.tile([P, KINDS, TILES_PER_IMAGE], F32)
+        nc.gpsimd.tensor_tensor(out=gate_w[:, 0:KINDS:2, :], in0=by_image(inv[:]), in1=by_image(blend[:]), op=ALU.mult)
+        nc.gpsimd.tensor_tensor(out=gate_w[:, 1:KINDS:2, :], in0=by_image(scaled[:]), in1=by_image(m[:]), op=ALU.mult)
 
         def piece_columns(piece):
             by_kind = weight_cols[:, 0:GATE_ROWS].rearrange("p (k c i) -> p k c i", k=KINDS, c=PIECES)
             return by_kind[:, :, piece, :]
 
-        def cut_piece(piece):
-            nc.vector.tensor_copy(out=piece_columns(piece), in_=rests[piece][:])
-
-        def take_rest(piece):
-            smaller = keep.tile([P, KINDS, TILES_PER_IMAGE], F32, name="rest_%d" % piece)
-            nc.vector.tensor_tensor(out=smaller[:], in0=rests[piece][:], in1=piece_columns(piece), op=ALU.subtract)
-            rests.append(smaller)
+        rest = keep.tile([P, KINDS, TILES_PER_IMAGE], F32)
+        nc.gpsimd.tensor_copy(out=piece_columns(0), in_=gate_w[:])
+        nc.gpsimd.tensor_tensor(out=rest[:], in0=gate_w[:], in1=piece_columns(0), op=ALU.subtract)
+        nc.gpsimd.tensor_copy(out=piece_columns(1), in_=rest[:])
+        nc.gpsimd.tensor_tensor(out=piece_columns(2), in0=rest[:], in1=piece_columns(1), op=ALU.subtract)
 
         def spread(row, name):
             bias_all = keep.tile([P, CHANNELS], BF16, name=name)
@@ -328,15 +323,10 @@ def tile_hydraattention_pb_kernel(
             if first <= tile_no < TILES:
                 stage(tile_no)
 
-        regroup_x(0)
-        cut_piece(0)
-        quantise_x(0)
-        regroup_x(1)
-        take_rest(0)
-        quantise_x(1)
-        cut_piece(1)
-        take_rest(1)
-        cut_piece(2)
+        for tile_no in range(TILES_PER_CHUNK):
+            regroup_x(tile_no)
+        for tile_no in range(TILES_PER_CHUNK):
+            quantise_x(tile_no)
 
         for s in range(FIRST_STEP, TILES + 2):
             run(outputs_mm, s - 2)

@@ -32,6 +32,7 @@ KINDS = 2 * IMAGES
 ROWS_PER_KIND = PIECES * TILES_PER_IMAGE
 GATE_ROWS = KINDS * ROWS_PER_KIND
 FIRST_STEP = -2
+VECTOR_ALONE = 2
 
 FLOPS = 2 * 2 * IMAGES * PIXELS * CHANNELS * CHANNELS
 
@@ -212,33 +213,34 @@ def tile_hydraattention_pb_kernel(
         def quantise_x(tile_no):
             x_mx[tile_no] = quantise(x_grouped_of[tile_no][:].rearrange("p g w j -> p (g w j)"), "x")
 
-        def project(operand, weight):
+        def project(operand, weight, width=BANK):
             codes, scales = operand
             words, planes = weight
-            banks = []
+            groups = []
             for half in range(HALVES):
                 acc = psum.tile([P, BANK], F32, bufs=4)
-                for g in range(GROUPS):
-                    nc.tensor.matmul_mx(
-                        out=acc[:],
-                        lhsT=codes[:, g * P : (g + 1) * P].bitcast(FP8X4),
-                        lhsT_scale=scales[:, g * P : (g + 1) * P],
-                        rhs=words[:, g, half_cols(half)].bitcast(FP8X4),
-                        rhs_scale=planes[PLANE_ROWS * g : P, half_cols(half)],
-                        start=(g == 0),
-                        stop=(g == GROUPS - 1),
-                    )
-                banks.append(acc)
-            return banks
+                for first in range(0, BANK, width):
+                    cols = slice(half * BANK + first, half * BANK + first + width)
+                    for g in range(GROUPS):
+                        nc.tensor.matmul_mx(
+                            out=acc[:, first : first + width],
+                            lhsT=codes[:, g * P : (g + 1) * P].bitcast(FP8X4),
+                            lhsT_scale=scales[:, g * P : (g + 1) * P],
+                            rhs=words[:, g, cols].bitcast(FP8X4),
+                            rhs_scale=planes[PLANE_ROWS * g : P, cols],
+                            start=(g == 0),
+                            stop=(g == GROUPS - 1),
+                        )
+                    groups.append((acc[:, first : first + width], cols))
+            return groups
 
         def queries_mm(tile_no):
             q_banks[tile_no] = project(x_mx[tile_no], w_q)
 
         def queries_exit(tile_no):
             q = work.tile([P, CHANNELS], F32)
-            for half in range(HALVES):
-                cols = half_cols(half)
-                nc.vector.tensor_tensor(out=q[:, cols], in0=q_banks[tile_no][half][:], in1=bq_all[:, cols], op=ALU.add)
+            for acc, cols in q_banks[tile_no]:
+                nc.vector.tensor_tensor(out=q[:, cols], in0=acc, in1=bq_all[:, cols], op=ALU.add)
             squares = work.tile([P, CHANNELS], BF16)
             sum_sq = small.tile([P, 1], F32)
             nc.scalar.activation(out=squares[:], in_=q[:], func=ACT.Square, accum_out=sum_sq[:])
@@ -303,21 +305,19 @@ def tile_hydraattention_pb_kernel(
             g_mx[tile_no] = quantise(g_grouped_of[tile_no][:], "g")
 
         def outputs_mm(tile_no):
-            y_banks[tile_no] = project(g_mx[tile_no], w_out)
+            y_banks[tile_no] = project(g_mx[tile_no], w_out, BANK // 2 if tile_no == TILES - 1 else BANK)
 
         def outputs_exit(tile_no):
             image, in_image = divmod(tile_no, TILES_PER_IMAGE)
             rows = out[image, in_image * P : (in_image + 1) * P, :]
-            first, second = half_cols(0), half_cols(1)
             y = work.tile([P, CHANNELS], F32)
-            nc.vector.tensor_tensor(out=y[:, first], in0=y_banks[tile_no][0][:], in1=bo_all[:, first], op=ALU.add)
-            nc.sync.dma_start(out=rows[:, first], in_=y[:, first])
-            if tile_no == TILES - 1:
-                nc.vector.tensor_tensor(out=y[:, second], in0=y_banks[tile_no][1][:], in1=bo_all[:, second], op=ALU.add)
-            else:
-                nc.scalar.copy(out=y[:, second], in_=y_banks[tile_no][1][:])
-                nc.gpsimd.tensor_tensor(out=y[:, second], in0=y[:, second], in1=bo_all[:, second], op=ALU.add)
-            nc.sync.dma_start(out=rows[:, second], in_=y[:, second])
+            for number, (acc, cols) in enumerate(y_banks[tile_no]):
+                if number == 0 or tile_no >= TILES - VECTOR_ALONE:
+                    nc.vector.tensor_tensor(out=y[:, cols], in0=acc, in1=bo_all[:, cols], op=ALU.add)
+                else:
+                    nc.scalar.copy(out=y[:, cols], in_=acc)
+                    nc.gpsimd.tensor_tensor(out=y[:, cols], in0=y[:, cols], in1=bo_all[:, cols], op=ALU.add)
+                nc.sync.dma_start(out=rows[:, cols], in_=y[:, cols])
 
         def run(stage, tile_no, first=0):
             if first <= tile_no < TILES:

@@ -331,12 +331,12 @@ def tile_hydraattention_pb_kernel(
         for s in range(FIRST_STEP, TILES + 2):
             run(outputs_mm, s - 2)
             run(queries_exit, s + 1)
-            run(regroup_x, s + 4)
             run(queries_mm, s + 2)
             run(gate_apply, s)
             run(gate_mm, s + 1)
             run(quantise_g, s - 1)
             run(outputs_exit, s - 2)
+            run(regroup_x, s + 4)
             run(turn, s)
             if s == FIRST_STEP:
                 turn_weights()

@@ -32,6 +32,7 @@ KINDS = 2 * IMAGES
 ROWS_PER_KIND = PIECES * TILES_PER_IMAGE
 GATE_ROWS = KINDS * ROWS_PER_KIND
 FIRST_STEP = -2
+X_AHEAD = 4
 VECTOR_ALONE = 2
 
 FLOPS = 2 * 2 * IMAGES * PIXELS * CHANNELS * CHANNELS
@@ -180,41 +181,49 @@ def tile_hydraattention_pb_kernel(
         bq_all = spread(0, "bq_all")
         bo_all = spread(1, "bo_all")
 
-        x_grouped_of = {}
+        staged_of = {}
         x_mx = {}
         q_banks = {}
         q_of = {}
         weight_rows_of = {}
         gate_banks = {}
         g_rows_of = {}
-        g_grouped_of = {}
         g_mx = {}
         y_banks = {}
+
+        def staged(step):
+            if step not in staged_of:
+                staged_of[step] = work.tile([P, 2, CHANNELS], BF16, name="staged", align_bytes=64)
+            return staged_of[step]
 
         def regroup_x(tile_no):
             image, in_image = divmod(tile_no, TILES_PER_IMAGE)
             chunk, in_chunk = divmod(in_image, TILES_PER_CHUNK)
             pixels = slice(in_chunk * P, (in_chunk + 1) * P)
             copy = nc.vector.tensor_copy if tile_no < TILES_PER_CHUNK else nc.scalar.copy
-            x_grouped = work.tile([P, GROUPS, P, PACK], BF16, align_bytes=64)
+            x_grouped = staged(tile_no - X_AHEAD)[:, 1].rearrange("p (g w j) -> p g w j", g=GROUPS, j=PACK)
             for g in range(GROUPS):
                 copy(
                     out=x_grouped[:, g].rearrange("p (c i) j -> p c j i", i=4),
                     in_=x_raw[(image, chunk, g)][:, :, pixels].rearrange("p j (c i) -> p c j i", i=4),
                 )
-            x_grouped_of[tile_no] = x_grouped
 
-        def quantise(grouped, what):
-            codes = work.tile([P, GROUPS * P], U32, tag=what + "_codes", align_bytes=64)
-            scales = work.tile([P, GROUPS * P], U8, tag=what + "_scales", align_bytes=64)
-            nc.vector.quantize_mx(out=codes[:].bitcast(FP8X4), scales=scales[:], in_=grouped)
-            return codes, scales
-
-        def quantise_x(tile_no):
-            x_mx[tile_no] = quantise(x_grouped_of[tile_no][:].rearrange("p g w j -> p (g w j)"), "x")
+        def quantise(step):
+            words = GROUPS * P
+            codes = work.tile([P, 2 * words], U32, align_bytes=64)
+            scales = work.tile([P, 2 * words], U8, align_bytes=64)
+            present = [slot for slot, tile_no in enumerate((step, step + X_AHEAD)) if 0 <= tile_no < TILES]
+            first, end = present[0], present[-1] + 1
+            nc.vector.quantize_mx(
+                out=codes[:, first * words : end * words].bitcast(FP8X4),
+                scales=scales[:, first * words : end * words],
+                in_=staged(step)[:, first:end].rearrange("p s c -> p (s c)"),
+            )
+            g_mx[step] = (codes, scales, 0)
+            x_mx[step + X_AHEAD] = (codes, scales, words)
 
         def project(operand, weight, width=BANK):
-            codes, scales = operand
+            codes, scales, first_word = operand
             words, planes = weight
             groups = []
             for half in range(HALVES):
@@ -224,8 +233,8 @@ def tile_hydraattention_pb_kernel(
                     for g in range(GROUPS):
                         nc.tensor.matmul_mx(
                             out=acc[:, first : first + width],
-                            lhsT=codes[:, g * P : (g + 1) * P].bitcast(FP8X4),
-                            lhsT_scale=scales[:, g * P : (g + 1) * P],
+                            lhsT=codes[:, first_word + g * P : first_word + (g + 1) * P].bitcast(FP8X4),
+                            lhsT_scale=scales[:, first_word + g * P : first_word + (g + 1) * P],
                             rhs=words[:, g, cols].bitcast(FP8X4),
                             rhs_scale=planes[PLANE_ROWS * g : P, cols],
                             start=(g == 0),
@@ -294,15 +303,10 @@ def tile_hydraattention_pb_kernel(
                     nc.tensor.transpose(
                         turned[:, g, u, :], pairs[:, g * pair_cols + u : (g + 1) * pair_cols : 2], ident_f32[:]
                     )
-            g_grouped = work.tile([P, CHANNELS], BF16, align_bytes=64)
             nc.scalar.copy(
-                out=g_grouped[:].bitcast(F32).rearrange("p (g w u) -> p g w u", g=GROUPS, u=2),
+                out=staged(tile_no)[:, 0].bitcast(F32).rearrange("p (g w u) -> p g w u", g=GROUPS, u=2),
                 in_=turned[:].rearrange("p g u w -> p g w u"),
             )
-            g_grouped_of[tile_no] = g_grouped
-
-        def quantise_g(tile_no):
-            g_mx[tile_no] = quantise(g_grouped_of[tile_no][:], "g")
 
         def outputs_mm(tile_no):
             y_banks[tile_no] = project(g_mx[tile_no], w_out, BANK // 2 if tile_no == TILES - 1 else BANK)
@@ -326,7 +330,7 @@ def tile_hydraattention_pb_kernel(
         for tile_no in range(TILES_PER_CHUNK):
             regroup_x(tile_no)
         for tile_no in range(TILES_PER_CHUNK):
-            quantise_x(tile_no)
+            quantise(tile_no - X_AHEAD)
 
         for s in range(FIRST_STEP, TILES + 2):
             run(outputs_mm, s - 2)
@@ -334,11 +338,11 @@ def tile_hydraattention_pb_kernel(
             run(queries_mm, s + 2)
             run(gate_apply, s)
             run(gate_mm, s + 1)
-            run(quantise_g, s - 1)
+            if FIRST_STEP <= s - 1 < TILES:
+                quantise(s - 1)
             run(outputs_exit, s - 2)
-            run(regroup_x, s + 4)
+            run(regroup_x, s + X_AHEAD)
             run(turn, s)
             if s == FIRST_STEP:
                 turn_weights()
             run(weights, s + 2)
-            run(quantise_x, s + 3, first=TILES_PER_CHUNK)

@@ -29,7 +29,8 @@ TILES_PER_CHUNK = CHUNK // P
 PIECES = 3
 PLANE_ROWS = 4
 KINDS = 2 * IMAGES
-ROWS_PER_KIND = PIECES * TILES_PER_IMAGE
+PLACES = 4
+ROWS_PER_KIND = PLACES * TILES_PER_IMAGE
 GATE_ROWS = KINDS * ROWS_PER_KIND
 FIRST_STEP = -2
 X_AHEAD = 4
@@ -110,7 +111,6 @@ def tile_hydraattention_pb_kernel(
         nc.vector.memset(weight_cols[:].bitcast(I32), 0)
 
         kv_rows = keep.tile([P, CHANNELS], BF16)
-        nc.gpsimd.memset(kv_rows[:], 0.0)
 
         def load_kv(image):
             for which, vector in enumerate((kv_know, kv_mask)):
@@ -160,7 +160,7 @@ def tile_hydraattention_pb_kernel(
         nc.gpsimd.tensor_tensor(out=gate_w[:, 1:KINDS:2, :], in0=by_image(scaled[:]), in1=by_image(m[:]), op=ALU.mult)
 
         def piece_columns(piece):
-            by_kind = weight_cols[:, 0:GATE_ROWS].rearrange("p (k c i) -> p k c i", k=KINDS, c=PIECES)
+            by_kind = weight_cols[:, 0:GATE_ROWS].rearrange("p (k c i) -> p k c i", k=KINDS, c=PLACES)
             return by_kind[:, :, piece, :]
 
         rest = keep.tile([P, KINDS, TILES_PER_IMAGE], F32)

@@ -272,16 +272,13 @@ def tile_hydraattention_pb_kernel(
             )
             weight_rows_of[tile_no] = weight_rows
 
-        def gate_mm(tile_no):
-            banks = []
-            for half in range(HALVES):
-                gate_ps = psum.tile([P, BANK], F32)
-                nc.tensor.matmul(
-                    out=gate_ps[:], lhsT=weight_rows_of[tile_no][:], rhs=kv_rows[:, half_cols(half)],
-                    start=True, stop=True,
-                )
-                banks.append(gate_ps)
-            gate_banks[tile_no] = banks
+        def gate_mm(tile_no, half):
+            gate_ps = psum.tile([P, BANK], F32)
+            nc.tensor.matmul(
+                out=gate_ps[:], lhsT=weight_rows_of[tile_no][:], rhs=kv_rows[:, half_cols(half)],
+                start=True, stop=True,
+            )
+            gate_banks[(tile_no, half)] = gate_ps
 
         def gate_apply(tile_no):
             q, inv_norm = q_of[tile_no]
@@ -289,7 +286,7 @@ def tile_hydraattention_pb_kernel(
             for half in range(HALVES):
                 cols = half_cols(half)
                 nc.vector.scalar_tensor_tensor(
-                    out=g_rows[:, cols], in0=q[:, cols], scalar=inv_norm[:, 0:1], in1=gate_banks[tile_no][half][:],
+                    out=g_rows[:, cols], in0=q[:, cols], scalar=inv_norm[:, 0:1], in1=gate_banks[(tile_no, half)][:],
                     op0=ALU.mult, op1=ALU.mult,
                 )
             g_rows_of[tile_no] = g_rows
@@ -323,9 +320,9 @@ def tile_hydraattention_pb_kernel(
                     nc.gpsimd.tensor_tensor(out=y[:, cols], in0=y[:, cols], in1=bo_all[:, cols], op=ALU.add)
                 nc.sync.dma_start(out=rows[:, cols], in_=y[:, cols])
 
-        def run(stage, tile_no, first=0):
-            if first <= tile_no < TILES:
-                stage(tile_no)
+        def run(stage, tile_no, *which):
+            if 0 <= tile_no < TILES:
+                stage(tile_no, *which)
 
         for tile_no in range(TILES_PER_CHUNK):
             regroup_x(tile_no)
@@ -337,12 +334,13 @@ def tile_hydraattention_pb_kernel(
             run(queries_exit, s + 1)
             run(queries_mm, s + 2)
             run(gate_apply, s)
-            run(gate_mm, s + 1)
+            run(gate_mm, s + 1, 0)
             if FIRST_STEP <= s - 1 < TILES:
                 quantise(s - 1)
             run(outputs_exit, s - 2)
             run(regroup_x, s + X_AHEAD)
             run(turn, s)
+            run(gate_mm, s + 1, 1)
             if s == FIRST_STEP:
                 turn_weights()
             run(weights, s + 2)

@@ -34,7 +34,9 @@ ROWS_PER_KIND = PLACES * TILES_PER_IMAGE
 GATE_ROWS = KINDS * ROWS_PER_KIND
 FIRST_STEP = -2
 X_AHEAD = 4
-VECTOR_ALONE = 2
+VECTOR_ALONE = 4
+VECTOR_REGROUPS = 3
+WEIGHTS_A_STEP = 3
 
 FLOPS = 2 * 2 * IMAGES * PIXELS * CHANNELS * CHANNELS
 
@@ -200,7 +202,7 @@ def tile_hydraattention_pb_kernel(
             image, in_image = divmod(tile_no, TILES_PER_IMAGE)
             chunk, in_chunk = divmod(in_image, TILES_PER_CHUNK)
             pixels = slice(in_chunk * P, (in_chunk + 1) * P)
-            copy = nc.vector.tensor_copy if tile_no < TILES_PER_CHUNK else nc.scalar.copy
+            copy = nc.vector.tensor_copy if tile_no < VECTOR_REGROUPS else nc.scalar.copy
             x_grouped = staged(tile_no - X_AHEAD)[:, 1].rearrange("p (g w j) -> p g w j", g=GROUPS, j=PACK)
             for g in range(GROUPS):
                 copy(
@@ -265,7 +267,7 @@ def tile_hydraattention_pb_kernel(
             nc.scalar.copy(out=all_weight_rows[:], in_=weight_ps[:, 0:P])
 
         def weights(tile_no):
-            weight_rows = work.tile([P, P], BF16)
+            weight_rows = work.tile([P, P], BF16, bufs=TILES)
             nc.gpsimd.tensor_scalar(
                 out=weight_rows[:], in0=all_weight_rows[:], scalar1=tile_rows[:, tile_no : tile_no + 1], scalar2=0.0,
                 op0=ALU.mult, op1=ALU.add,
@@ -332,15 +334,20 @@ def tile_hydraattention_pb_kernel(
         for s in range(FIRST_STEP, TILES + 2):
             run(outputs_mm, s - 2)
             run(queries_exit, s + 1)
+            if s == -1:
+                regroup_x(VECTOR_REGROUPS - 1)
             run(queries_mm, s + 2)
             run(gate_apply, s)
             run(gate_mm, s + 1, 0)
             if FIRST_STEP <= s - 1 < TILES:
                 quantise(s - 1)
             run(outputs_exit, s - 2)
-            run(regroup_x, s + X_AHEAD)
+            if s + X_AHEAD >= VECTOR_REGROUPS:
+                run(regroup_x, s + X_AHEAD)
             run(turn, s)
             run(gate_mm, s + 1, 1)
             if s == FIRST_STEP:
                 turn_weights()
-            run(weights, s + 2)
+            made = 2 + WEIGHTS_A_STEP * (s - FIRST_STEP)
+            for tile_no in range(max(0, made - WEIGHTS_A_STEP) if s > FIRST_STEP else 0, made):
+                run(weights, tile_no)

@@ -36,6 +36,7 @@ FIRST_STEP = -2
 X_AHEAD = 4
 VECTOR_ALONE = 4
 VECTOR_REGROUPS = 3
+RUN = 8
 WEIGHTS_A_STEP = 3
 
 FLOPS = 2 * 2 * IMAGES * PIXELS * CHANNELS * CHANNELS
@@ -206,8 +207,8 @@ def tile_hydraattention_pb_kernel(
             x_grouped = staged(tile_no - X_AHEAD)[:, 1].rearrange("p (g w j) -> p g w j", g=GROUPS, j=PACK)
             for g in range(GROUPS):
                 copy(
-                    out=x_grouped[:, g].rearrange("p (c i) j -> p c j i", i=4),
-                    in_=x_raw[(image, chunk, g)][:, :, pixels].rearrange("p j (c i) -> p c j i", i=4),
+                    out=x_grouped[:, g].rearrange("p (c i) j -> p c j i", i=RUN),
+                    in_=x_raw[(image, chunk, g)][:, :, pixels].rearrange("p j (c i) -> p c j i", i=RUN),
                 )
 
         def quantise(step):

from contextlib import ExitStack

import concourse.mybir as mybir
from concourse.masks import make_identity

F32 = mybir.dt.float32
BF16 = mybir.dt.bfloat16
I32 = mybir.dt.int32
U32 = mybir.dt.uint32
U8 = mybir.dt.uint8
FP8X4 = mybir.dt.float8_e4m3fn_x4
ALU = mybir.AluOpType
ACT = mybir.ActivationFunctionType

P = 128
PACK = 4
K_PASS = P * PACK
IMAGES = 2
PIXELS = 1024
CHANNELS = 1024
GROUPS = CHANNELS // K_PASS
BANK = 512
HALVES = CHANNELS // BANK
TILES_PER_IMAGE = PIXELS // P
TILES = IMAGES * TILES_PER_IMAGE
CHUNK = 256
CHUNKS = PIXELS // CHUNK
TILES_PER_CHUNK = CHUNK // P
PIECES = 3
PLANE_ROWS = 4
KINDS = 2 * IMAGES
PLACES = 4
ROWS_PER_KIND = PLACES * TILES_PER_IMAGE
GATE_ROWS = KINDS * ROWS_PER_KIND
FIRST_STEP = -2
X_AHEAD = 4
VECTOR_ALONE = 4
VECTOR_REGROUPS = 3
RUN = 8
WEIGHTS_A_STEP = 3

FLOPS = 2 * 2 * IMAGES * PIXELS * CHANNELS * CHANNELS


def half_cols(half):
    return slice(half * BANK, (half + 1) * BANK)


def tile_hydraattention_pb_kernel(
    tc, x, mask, W_q_words, W_q_scales, b_q, kv_know, kv_mask, W_out_words, W_out_scales, b_out, out
):
    nc = tc.nc
    with ExitStack() as ctx:
        keep = ctx.enter_context(tc.tile_pool(name="keep", bufs=1))
        small = ctx.enter_context(tc.tile_pool(name="small", bufs=4))
        work = ctx.enter_context(tc.tile_pool(name="work", bufs=3))
        psum = ctx.enter_context(tc.psum_pool(name="psum", bufs=2))
        ctx.enter_context(tc.manual_schedule())

        minus_half = keep.tile([P, 1], F32)
        nc.vector.memset(minus_half[:], -0.5)
        warm = keep.tile([P, 1], F32)
        nc.scalar.activation(out=warm[:], in_=minus_half[:], func=ACT.Square)


        def weight_tiles(name):
            words = keep.tile([P, GROUPS, CHANNELS], U32, name=name + "_words", align_bytes=64)
            planes = keep.tile([P, CHANNELS], U8, name=name + "_planes", align_bytes=64)
            nc.vector.memset(planes[:].bitcast(I32), 0)
            return words, planes

        def load_planes(weight, scales_in):
            planes = weight[1]
            for quadrant in range(4):
                nc.sync.dma_start(
                    out=planes[32 * quadrant : 32 * quadrant + GROUPS * PLANE_ROWS, :].bitcast(I32),
                    in_=scales_in[:, PLANE_ROWS * quadrant : PLANE_ROWS * (quadrant + 1), :].bitcast(I32),
                )

        def load_words(weight, words_in, half):
            nc.sync.dma_start(
                out=weight[0][:, :, half_cols(half)].bitcast(I32),
                in_=words_in[:, :, half_cols(half), :].rearrange("g p n t -> p g (n t)").bitcast(I32),
            )

        x_raw = {}

        def load_x(image, chunk):
            for g in range(GROUPS):
                raw = keep.tile([P, PACK, CHUNK], BF16, name="x_raw_%d_%d_%d" % (image, chunk, g))
                rows = x[image, g * K_PASS : (g + 1) * K_PASS].rearrange("(p j) r w -> p j (r w)", j=PACK)
                nc.sync.dma_start(out=raw[:], in_=rows[:, :, chunk * CHUNK : (chunk + 1) * CHUNK])
                x_raw[(image, chunk, g)] = raw

        load_x(0, 0)
        bias_rows = keep.tile([P, CHANNELS], BF16)
        nc.vector.memset(bias_rows[:].bitcast(I32), 0)
        nc.sync.dma_start(out=bias_rows[0:1, :], in_=b_q.unsqueeze(0))
        nc.sync.dma_start(out=bias_rows[1:2, :], in_=b_out.unsqueeze(0))
        mask_rows = keep.tile([P, P], BF16)
        nc.vector.memset(mask_rows[:].bitcast(I32), 0)
        nc.sync.dma_start(
            out=mask_rows[0:TILES, :],
            in_=mask.rearrange("b o (i r) w -> (b o i) (r w)", i=TILES_PER_IMAGE),
        )
        w_q = weight_tiles("wq")
        load_words(w_q, W_q_words, 0)
        load_planes(w_q, W_q_scales)
        load_words(w_q, W_q_words, 1)

        ident_bf = keep.tile([P, P], BF16)
        make_identity(nc, ident_bf[:])
        weight_cols = keep.tile([P, P], BF16)
        nc.vector.memset(weight_cols[:].bitcast(I32), 0)

        kv_rows = keep.tile([P, CHANNELS], BF16)

        def load_kv(image):
            for which, vector in enumerate((kv_know, kv_mask)):
                first = (2 * image + which) * ROWS_PER_KIND
                nc.sync.dma_start(
                    out=kv_rows[first : first + ROWS_PER_KIND, :], in_=vector[image, 0].partition_broadcast(ROWS_PER_KIND)
                )

        load_x(0, 1)
        load_kv(0)
        load_kv(1)
        load_x(0, 2)
        w_out = weight_tiles("wo")
        load_words(w_out, W_out_words, 0)
        load_planes(w_out, W_out_scales)
        load_words(w_out, W_out_words, 1)
        load_x(0, 3)
        for chunk in range(CHUNKS):
            load_x(1, chunk)

        ident_f32 = keep.tile([P, P], F32)
        make_identity(nc, ident_f32[:])

        mask_ps = psum.tile([P, 2 * BANK], BF16, tag="turned")
        nc.tensor.transpose(mask_ps[:, 0:P], mask_rows[:], ident_bf[:])
        m = keep.tile([P, TILES], F32)
        nc.scalar.copy(out=m[:], in_=mask_ps[:, 0:TILES])

        def by_image(ap):
            return ap.rearrange("p (b i) -> p b i", b=IMAGES)

        tile_rows = keep.tile([P, TILES], F32)
        nc.vector.tensor_reduce(
            out=by_image(tile_rows[:]),
            in_=ident_bf[:, 0:GATE_ROWS].rearrange("p (b k i) -> p b i k", b=IMAGES, i=TILES_PER_IMAGE),
            axis=mybir.AxisListType.X, op=ALU.add,
        )

        inv = keep.tile([P, TILES], F32)
        nc.gpsimd.tensor_scalar(out=inv[:], in0=m[:], scalar1=-1.0, scalar2=1.0, op0=ALU.mult, op1=ALU.add)
        blend = keep.tile([P, TILES], F32)
        nc.gpsimd.tensor_scalar(out=blend[:], in0=m[:], scalar1=-0.7, scalar2=1.0, op0=ALU.mult, op1=ALU.add)
        scaled = keep.tile([P, TILES], F32)
        nc.gpsimd.tensor_scalar(out=scaled[:], in0=m[:], scalar1=0.7, scalar2=0.0, op0=ALU.mult, op1=ALU.add)
        gate_w = keep.tile([P, KINDS, TILES_PER_IMAGE], F32)
        nc.gpsimd.tensor_tensor(out=gate_w[:, 0:KINDS:2, :], in0=by_image(inv[:]), in1=by_image(blend[:]), op=ALU.mult)
        nc.gpsimd.tensor_tensor(out=gate_w[:, 1:KINDS:2, :], in0=by_image(scaled[:]), in1=by_image(m[:]), op=ALU.mult)

        def piece_columns(piece):
            by_kind = weight_cols[:, 0:GATE_ROWS].rearrange("p (k c i) -> p k c i", k=KINDS, c=PLACES)
            return by_kind[:, :, piece, :]

        rest = keep.tile([P, KINDS, TILES_PER_IMAGE], F32)
        nc.gpsimd.tensor_copy(out=piece_columns(0), in_=gate_w[:])
        nc.gpsimd.tensor_tensor(out=rest[:], in0=gate_w[:], in1=piece_columns(0), op=ALU.subtract)
        nc.gpsimd.tensor_copy(out=piece_columns(1), in_=rest[:])
        nc.gpsimd.tensor_tensor(out=piece_columns(2), in0=rest[:], in1=piece_columns(1), op=ALU.subtract)

        def spread(row, name):
            bias_all = keep.tile([P, CHANNELS], BF16, name=name)
            pick = ident_bf[:, row : row + 1].to_broadcast([P, P])
            for half in range(HALVES):
                bias_ps = psum.tile([P, BANK], F32, tag="gate_ps")
                nc.tensor.matmul(out=bias_ps[:], lhsT=pick, rhs=bias_rows[:, half_cols(half)], start=True, stop=True)
                nc.scalar.copy(out=bias_all[:, half_cols(half)], in_=bias_ps[:])
            return bias_all

        bq_all = spread(0, "bq_all")
        bo_all = spread(1, "bo_all")

        staged_of = {}
        x_mx = {}
        q_banks = {}
        q_of = {}
        weight_rows_of = {}
        gate_banks = {}
        g_rows_of = {}
        g_mx = {}
        y_banks = {}

        def staged(step):
            if step not in staged_of:
                staged_of[step] = work.tile([P, 2, CHANNELS], BF16, name="staged", align_bytes=64)
            return staged_of[step]

        def regroup_x(tile_no):
            image, in_image = divmod(tile_no, TILES_PER_IMAGE)
            chunk, in_chunk = divmod(in_image, TILES_PER_CHUNK)
            pixels = slice(in_chunk * P, (in_chunk + 1) * P)
            copy = nc.vector.tensor_copy if tile_no < VECTOR_REGROUPS else nc.scalar.copy
            x_grouped = staged(tile_no - X_AHEAD)[:, 1].rearrange("p (g w j) -> p g w j", g=GROUPS, j=PACK)
            for g in range(GROUPS):
                copy(
                    out=x_grouped[:, g].rearrange("p (c i) j -> p c j i", i=RUN),
                    in_=x_raw[(image, chunk, g)][:, :, pixels].rearrange("p j (c i) -> p c j i", i=RUN),
                )

        def quantise(step):
            words = GROUPS * P
            codes = work.tile([P, 2 * words], U32, align_bytes=64)
            scales = work.tile([P, 2 * words], U8, align_bytes=64)
            present = [slot for slot, tile_no in enumerate((step, step + X_AHEAD)) if 0 <= tile_no < TILES]
            first, end = present[0], present[-1] + 1
            nc.vector.quantize_mx(
                out=codes[:, first * words : end * words].bitcast(FP8X4),
                scales=scales[:, first * words : end * words],
                in_=staged(step)[:, first:end].rearrange("p s c -> p (s c)"),
            )
            g_mx[step] = (codes, scales, 0)
            x_mx[step + X_AHEAD] = (codes, scales, words)

        def project(operand, weight, width=BANK):
            codes, scales, first_word = operand
            words, planes = weight
            groups = []
            for half in range(HALVES):
                acc = psum.tile([P, BANK], F32, bufs=4)
                for first in range(0, BANK, width):
                    cols = slice(half * BANK + first, half * BANK + first + width)
                    for g in range(GROUPS):
                        nc.tensor.matmul_mx(
                            out=acc[:, first : first + width],
                            lhsT=codes[:, first_word + g * P : first_word + (g + 1) * P].bitcast(FP8X4),
                            lhsT_scale=scales[:, first_word + g * P : first_word + (g + 1) * P],
                            rhs=words[:, g, cols].bitcast(FP8X4),
                            rhs_scale=planes[PLANE_ROWS * g : P, cols],
                            start=(g == 0),
                            stop=(g == GROUPS - 1),
                        )
                    groups.append((acc[:, first : first + width], cols))
            return groups

        def queries_mm(tile_no):
            q_banks[tile_no] = project(x_mx[tile_no], w_q)

        def queries_exit(tile_no):
            q = work.tile([P, CHANNELS], F32)
            for acc, cols in q_banks[tile_no]:
                nc.vector.tensor_tensor(out=q[:, cols], in0=acc, in1=bq_all[:, cols], op=ALU.add)
            squares = work.tile([P, CHANNELS], BF16)
            sum_sq = small.tile([P, 1], F32)
            nc.scalar.activation(out=squares[:], in_=q[:], func=ACT.Square, accum_out=sum_sq[:])
            inv_norm = small.tile([P, 1], F32)
            nc.gpsimd.tensor_tensor(out=inv_norm[:], in0=sum_sq[:], in1=minus_half[:], op=ALU.pow)
            q_of[tile_no] = (q, inv_norm)

        all_weight_rows = keep.tile([P, P], BF16)

        def turn_weights():
            weight_ps = psum.tile([P, 2 * BANK], BF16, tag="turned")
            nc.tensor.transpose(weight_ps[:, 0:P], weight_cols[:], ident_bf[:])
            nc.scalar.copy(out=all_weight_rows[:], in_=weight_ps[:, 0:P])

        def weights(tile_no):
            weight_rows = work.tile([P, P], BF16, bufs=TILES)
            nc.gpsimd.tensor_scalar(
                out=weight_rows[:], in0=all_weight_rows[:], scalar1=tile_rows[:, tile_no : tile_no + 1], scalar2=0.0,
                op0=ALU.mult, op1=ALU.add,
            )
            weight_rows_of[tile_no] = weight_rows

        def gate_mm(tile_no, half):
            gate_ps = psum.tile([P, BANK], F32)
            nc.tensor.matmul(
                out=gate_ps[:], lhsT=weight_rows_of[tile_no][:], rhs=kv_rows[:, half_cols(half)],
                start=True, stop=True,
            )
            gate_banks[(tile_no, half)] = gate_ps

        def gate_apply(tile_no):
            q, inv_norm = q_of[tile_no]
            g_rows = work.tile([P, CHANNELS], BF16)
            for half in range(HALVES):
                cols = half_cols(half)
                nc.vector.scalar_tensor_tensor(
                    out=g_rows[:, cols], in0=q[:, cols], scalar=inv_norm[:, 0:1], in1=gate_banks[(tile_no, half)][:],
                    op0=ALU.mult, op1=ALU.mult,
                )
            g_rows_of[tile_no] = g_rows

        def turn(tile_no):
            pairs = g_rows_of[tile_no][:].bitcast(F32)
            pair_cols = K_PASS // 2
            turned = psum.tile([P, GROUPS, 2, P], F32)
            for g in range(GROUPS):
                for u in range(2):
                    nc.tensor.transpose(
                        turned[:, g, u, :], pairs[:, g * pair_cols + u : (g + 1) * pair_cols : 2], ident_f32[:]
                    )
            nc.scalar.copy(
                out=staged(tile_no)[:, 0].bitcast(F32).rearrange("p (g w u) -> p g w u", g=GROUPS, u=2),
                in_=turned[:].rearrange("p g u w -> p g w u"),
            )

        def outputs_mm(tile_no):
            y_banks[tile_no] = project(g_mx[tile_no], w_out, BANK // 2 if tile_no == TILES - 1 else BANK)

        def outputs_exit(tile_no):
            image, in_image = divmod(tile_no, TILES_PER_IMAGE)
            rows = out[image, in_image * P : (in_image + 1) * P, :]
            y = work.tile([P, CHANNELS], F32)
            for number, (acc, cols) in enumerate(y_banks[tile_no]):
                if number == 0 or tile_no >= TILES - VECTOR_ALONE:
                    nc.vector.tensor_tensor(out=y[:, cols], in0=acc, in1=bo_all[:, cols], op=ALU.add)
                else:
                    nc.scalar.copy(out=y[:, cols], in_=acc)
                    nc.gpsimd.tensor_tensor(out=y[:, cols], in0=y[:, cols], in1=bo_all[:, cols], op=ALU.add)
                nc.sync.dma_start(out=rows[:, cols], in_=y[:, cols])

        def run(stage, tile_no, *which):
            if 0 <= tile_no < TILES:
                stage(tile_no, *which)

        for tile_no in range(TILES_PER_CHUNK):
            regroup_x(tile_no)
        for tile_no in range(TILES_PER_CHUNK):
            quantise(tile_no - X_AHEAD)

        for s in range(FIRST_STEP, TILES + 2):
            run(outputs_mm, s - 2)
            run(queries_exit, s + 1)
            if s == -1:
                regroup_x(VECTOR_REGROUPS - 1)
            run(queries_mm, s + 2)
            run(gate_apply, s)
            run(gate_mm, s + 1, 0)
            if FIRST_STEP <= s - 1 < TILES:
                quantise(s - 1)
            run(outputs_exit, s - 2)
            if s + X_AHEAD >= VECTOR_REGROUPS:
                run(regroup_x, s + X_AHEAD)
            run(turn, s)
            run(gate_mm, s + 1, 1)
            if s == FIRST_STEP:
                turn_weights()
            made = 2 + WEIGHTS_A_STEP * (s - FIRST_STEP)
            for tile_no in range(max(0, made - WEIGHTS_A_STEP) if s > FIRST_STEP else 0, made):
                run(weights, tile_no)
